import numpy as np
import ml_dtypes


def mxq(x, axis, fmt="e4m3"):
    dtype, down = {"e4m3": (ml_dtypes.float8_e4m3fn, 7), "e5m2": (ml_dtypes.float8_e5m2, 14)}[fmt]
    v = np.moveaxis(np.asarray(x, np.float32).astype(ml_dtypes.bfloat16).astype(np.float64), axis, -1)
    blocks = v.reshape(v.shape[:-1] + (-1, 32))
    amax = np.abs(blocks).max(-1, keepdims=True)
    byte = np.maximum(np.where(amax > 0, np.frexp(amax)[1] - 1 + 127, 0) - down, 1)
    scale = np.exp2(byte - 127.0)
    codes = (blocks / scale).astype(np.float32).astype(dtype).astype(np.float64)
    return np.moveaxis((codes * scale).reshape(v.shape), -1, axis)


WIDE = False


def mx_kscale(k):
    if not WIDE:
        return np.ones(k)
    levels = np.array([10, -10, 5, -5, 0])
    a = np.random.permutation(np.resize(levels, k // 512 * 4)).reshape(k // 512, 4)
    idx = np.arange(k)
    return np.exp2(a[idx // 512, idx % 128 // 32])


BF16 = ml_dtypes.bfloat16


def bf(x):
    return np.asarray(x, np.float32).astype(BF16)


def f64(x):
    return np.asarray(x).astype(np.float64)


B, N, C = 16, 16, 1024
BN_EPS = 1e-5


def bn(v):
    mean = v.mean(axis=(0, 2), keepdims=True)
    var = v.var(axis=(0, 2), keepdims=True)
    return (v - mean) / np.sqrt(var + BN_EPS)


def sigmoid(v):
    return 1.0 / (1.0 + np.exp(-v))


def softmax(v, axis):
    p = np.exp(v - v.max(axis=axis, keepdims=True))
    return p / p.sum(axis=axis, keepdims=True)


def draw_w(a, f):
    return bf(np.random.standard_normal((C, C)) * a / np.sqrt(C) / f[None, :])


def setup_inputs():
    s, t = mx_kscale(C), mx_kscale(C)
    s, t = s / s.max(), t / t.max()
    return {"x": bf(np.random.standard_normal((B, N, C)) * s),
            "edge": bf(np.random.standard_normal((B, N * N, C)) * t),
            "WA": draw_w(np.sqrt(2.0), s), "WB": draw_w(np.sqrt(2.0), s), "WE": draw_w(np.sqrt(2.0), t),
            "WU": draw_w(0.4, s), "WV": draw_w(0.5 * N, s)}


def reference(x, edge, WA, WB, WE, WU, WV):
    x, edge = f64(x), f64(edge)
    xq = mxq(x, 2, "e4m3")
    Vix = xq @ mxq(f64(WA), 1, "e4m3").T
    Vjx = xq @ mxq(f64(WB), 1, "e4m3").T
    e_proj = mxq(edge, 2, "e4m3") @ mxq(f64(WE), 1, "e4m3").T
    agg = np.repeat(Vix, N, axis=1) + np.tile(Vjx, (1, N, 1)) + e_proj
    edge_out = edge + np.maximum(bn(agg), 0.0)
    e = sigmoid(edge_out).reshape(B, N, N, C)
    e = softmax(e, 2).reshape(B, N * N, C)
    Ujx = np.tile(xq @ mxq(f64(WV), 1, "e4m3").T, (1, N, 1))
    Uix = xq @ mxq(f64(WU), 1, "e4m3").T
    msg = (e * Ujx).reshape(B, N, N, C).sum(axis=2)
    x_new = Uix + msg / N
    x_out = np.maximum(x + bn(x_new), 0.0)
    return x_out, edge_out

@@ -1,0 +1,429 @@
+from contextlib import ExitStack
+
+import concourse.mybir as mybir
+from concourse.masks import make_identity
+
+F32 = mybir.dt.float32
+BF16 = mybir.dt.bfloat16
+U32 = mybir.dt.uint32
+U8 = mybir.dt.uint8
+FP8X4 = mybir.dt.float8_e4m3fn_x4
+ALU = mybir.AluOpType
+ACTF = mybir.ActivationFunctionType
+AX = mybir.AxisListType
+
+P = 128
+C = 1024
+NJ = 16
+NT = 32
+HALF = 512
+EPS = 1e-5
+FLOPS = 2 * 1024 * 1024 * (4096 + 4 * 256)
+
+PIN = True
+S9_POOL_EVERY = 0
+
+
+def tile_graphmodel_pa_t_kernel(tc, x, edge, WA, WB, WE, WU, WV, out_0, out_1):
+    nc = tc.nc
+    with ExitStack() as ctx:
+        const = ctx.enter_context(tc.tile_pool(name="const", bufs=1))
+        stage = ctx.enter_context(tc.tile_pool(name="stage", bufs=2))
+        work = ctx.enter_context(tc.tile_pool(name="work", bufs=2))
+        small = ctx.enter_context(tc.tile_pool(name="small", bufs=3))
+        psum = ctx.enter_context(tc.psum_pool(name="psum", bufs=1))
+        if PIN:
+            ctx.enter_context(tc.manual_schedule())
+
+        xv = x.flatten_outer_dims().rearrange("(p h) c -> h p c", h=2)
+        o0 = out_0.flatten_outer_dims().rearrange("(p h) c -> h p c", h=2)
+        ev = edge.flatten_outer_dims().rearrange("(p h j) c -> h p j c", h=2, j=NJ)
+        o1 = out_1.flatten_outer_dims().rearrange("(p h j) c -> h p j c", h=2, j=NJ)
+        wdram = {"WA": WA, "WB": WB, "WE": WE, "WU": WU, "WV": WV}
+        wview = {}
+        for w in wdram:
+            wview[w] = wdram[w].rearrange("(a r p) k -> a p r k", a=4, r=2)
+
+        warm = const.tile([P, 1], F32, name="warm")
+        nc.vector.memset(warm[:], 0.0)
+        warm2 = const.tile([P, 1], F32, name="warm2")
+        nc.scalar.activation(out=warm2[:], in_=warm[:], func=ACTF.Exp)
+        mhalf = const.tile([P, 1], F32, name="mhalf")
+        nc.vector.memset(mhalf[:], -0.5)
+        ident = const.tile([P, P], F32, name="ident")
+        make_identity(nc, ident[:])
+        rsel = const.tile([P, 8], F32, name="rsel")
+        nc.vector.tensor_reduce(
+            out=rsel[:], in_=ident[:].rearrange("p (a r) -> p r a", r=8), axis=AX.X, op=ALU.add
+        )
+        negg = const.tile([P, P], F32, name="negg")
+        nc.vector.tensor_scalar(
+            out=negg[:].rearrange("p (a r) -> p a r", r=8),
+            in0=rsel[:].unsqueeze(1).to_broadcast([P, 16, 8]),
+            scalar1=-1.0 / 16.0,
+            scalar2=None,
+            op0=ALU.mult,
+        )
+
+        wc = {}
+        ws = {}
+        for w in wdram:
+            wc[w] = const.tile([P, 2, C], U32, name="wc" + w, align_bytes=64)
+            ws[w] = const.tile([P, 2, C], U8, name="ws" + w, align_bytes=64)
+        xn = const.tile([P, 2, C], BF16, name="xn")
+        gx = const.tile([P, 2, 2, 512], BF16, name="gx", align_bytes=64)
+        xc = const.tile([P, 2, 2, P], U32, name="xc", align_bytes=64)
+        xs = const.tile([P, 2, 2, P], U8, name="xs", align_bytes=64)
+        xrc = const.tile([P, NJ, 2, P], U32, name="xrc", align_bytes=64)
+        xrs = const.tile([P, NJ, 2, P], U8, name="xrs", align_bytes=64)
+        den = [const.tile([P, C], F32, name="den%d" % h) for h in range(2)]
+        num = [const.tile([P, C], F32, name="num%d" % h) for h in range(2)]
+
+        def transposes(src_f32, tag, bufs):
+            bank = psum.tile([P, HALF], F32, name="bank_" + tag, tag=tag, bufs=bufs)
+            for blk in range(4):
+                cols = slice(blk * P, (blk + 1) * P)
+                nc.tensor.transpose(bank[:, cols], src_f32[:, cols], ident[:])
+            return bank
+
+        def regroup(dst_f32, bank):
+            nc.scalar.copy(out=dst_f32, in_=bank[:].rearrange("q (g u r) -> q g r u", g=2, u=2))
+
+        def mx(out, lc, ls, rc, rs, start, stop):
+            nc.tensor.matmul_mx(
+                out=out,
+                lhsT=lc.bitcast(FP8X4),
+                lhsT_scale=ls,
+                rhs=rc.bitcast(FP8X4),
+                rhs_scale=rs,
+                start=start,
+                stop=stop,
+            )
+
+        wn = {}
+
+        def load_w(w, a):
+            t = stage.tile([P, 2, C], BF16, name="wn", tag="wn", bufs=4)
+            nc.sync.dma_start(out=t[:], in_=wview[w][a])
+            wn[(w, a)] = t
+
+        ech = {}
+
+        def load_e(jc):
+            for h in range(2):
+                t = stage.tile([P, 2, C], BF16, name="ech", tag="ech", bufs=6)
+                nc.sync.dma_start(out=t[:], in_=ev[h][:, 2 * jc : 2 * jc + 2, :])
+                ech[(h, jc)] = t
+
+        for h in range(2):
+            nc.sync.dma_start(out=xn[:, h, :], in_=xv[h])
+        load_e(0)
+
+        gwt = {}
+
+        def prep_w(w, a, tags):
+            n2 = a // 2
+            if a % 2 == 0:
+                gwt[w] = stage.tile([P, 2, 2048], BF16, name="gw", tag="gw", bufs=3, align_bytes=64)
+            gwf = gwt[w][:].bitcast(F32).rearrange("q g (r u) -> q g r u", u=2)
+            wf = wn[(w, a)][:].bitcast(F32)
+            for r2 in range(2):
+                tag, bufs = tags[r2 % len(tags)]
+                bank = transposes(wf[:, r2, :], tag, bufs)
+                r0 = ((a % 2) * 2 + r2) * P
+                regroup(gwf[:, :, r0 : r0 + P, :], bank)
+            if a % 2 == 1:
+                cols = slice(n2 * HALF, (n2 + 1) * HALF)
+                for g in range(2):
+                    nc.vector.quantize_mx(
+                        out=wc[w][:, g, cols].bitcast(FP8X4),
+                        scales=ws[w][:, g, cols],
+                        in_=gwt[w][:, g, :],
+                    )
+
+        def prep_xrep(a):
+            grx = stage.tile([P, 4, 2, 512], BF16, name="grx", tag="gw", bufs=3, align_bytes=64)
+            grf = grx[:].bitcast(F32)
+            gxf = gx[:].bitcast(F32)
+            for jj in range(4):
+                j = 4 * a + jj
+                for g in range(2):
+                    src = gxf[:, j % 2, g, :].rearrange("q (b l u) -> q b l u", b=16, l=8)[:, :, j // 2, :]
+                    nc.vector.tensor_copy(
+                        out=grf[:, jj, g, :].rearrange("q (b i u) -> q b i u", b=16, i=8),
+                        in_=src.unsqueeze(2).to_broadcast([P, 16, 8, 2]),
+                    )
+            nc.vector.quantize_mx(
+                out=xrc[:, 4 * a : 4 * a + 4, :, :].rearrange("q j g r -> q (j g r)").bitcast(FP8X4),
+                scales=xrs[:, 4 * a : 4 * a + 4, :, :].rearrange("q j g r -> q (j g r)"),
+                in_=grx[:].rearrange("q j g w -> q (j g w)"),
+            )
+
+        start_tags = [("acc", 4), ("ub", 2)]
+        for n2 in range(2):
+            for w in ("WE", "WA", "WB"):
+                load_w(w, 2 * n2)
+                load_w(w, 2 * n2 + 1)
+                if n2 == 0 and w == "WE":
+                    gxf0 = gx[:].bitcast(F32)
+                    xf = xn[:].bitcast(F32)
+                    for h in range(2):
+                        bank = transposes(xf[:, h, :], "acc", 4)
+                        regroup(gxf0[:, h, :, :].rearrange("q g (r u) -> q g r u", u=2), bank)
+                    nc.vector.quantize_mx(
+                        out=xc[:].rearrange("q h g r -> q (h g r)").bitcast(FP8X4),
+                        scales=xs[:].rearrange("q h g r -> q (h g r)"),
+                        in_=gx[:].rearrange("q h g w -> q (h g w)"),
+                    )
+                    prep_xrep(0)
+                prep_w(w, 2 * n2, start_tags)
+                prep_w(w, 2 * n2 + 1, start_tags)
+        load_e(1)
+        for a in range(4):
+            load_w("WV", a)
+        load_e(2)
+
+        ge = {}
+        ecs = {}
+        trb = {}
+        acc = {}
+        stt_ = {}
+        nmt = {}
+        rstd = {}
+        rz = {}
+        et = {}
+        mt = {}
+        ubt = {}
+
+        def ok(t):
+            return 0 <= t < NT
+
+        def st_tr(t):
+            if not ok(t):
+                return
+            j, h = t // 2, t % 2
+            ef = ech[(h, j // 2)][:].bitcast(F32)
+            trb[t] = transposes(ef[:, j % 2, :], "tr", 1)
+
+        def st_evac(t):
+            if not ok(t):
+                return
+            ge[t] = stage.tile([P, 2, 512], BF16, name="ge", tag="ge", bufs=3, align_bytes=64)
+            regroup(ge[t][:].bitcast(F32).rearrange("q g (r u) -> q g r u", u=2), trb[t])
+
+        def st_q(t):
+            if not ok(t):
+                return
+            c_ = stage.tile([P, 2, P], U32, name="ec", tag="ec", bufs=4, align_bytes=64)
+            s_ = stage.tile([P, 2, P], U8, name="es", tag="es", bufs=4, align_bytes=64)
+            nc.vector.quantize_mx(
+                out=c_[:].rearrange("q g r -> q (g r)").bitcast(FP8X4),
+                scales=s_[:].rearrange("q g r -> q (g r)"),
+                in_=ge[t][:].rearrange("q g w -> q (g w)"),
+            )
+            ecs[t] = (c_, s_)
+
+        def st_c(t, n2):
+            if not ok(t):
+                return
+            j, h = t // 2, t % 2
+            a_ = psum.tile([P, HALF], F32, name="acc", tag="acc", bufs=4)
+            acc[(t, n2)] = a_
+            cols = slice(n2 * HALF, (n2 + 1) * HALF)
+            c_, s_ = ecs[t]
+            ops = [
+                (c_, s_, "WE"),
+                (xc[:, h], xs[:, h], "WA"),
+                (xrc[:, j], xrs[:, j], "WB"),
+            ]
+            i = 0
+            for lc, ls, w in ops:
+                for g in range(2):
+                    mx(a_[:], lc[:, g, :], ls[:, g, :], wc[w][:, g, cols], ws[w][:, g, cols], i == 0, i == 5)
+                    i += 1
+
+        def stats_a(key, srcs):
+            bst = small.tile([P, 12], F32, name="bst", tag="bst", bufs=3)
+            for n2 in range(2):
+                nc.vector.bn_stats(out=bst[:, 6 * n2 : 6 * n2 + 6], in_=srcs[n2])
+            mv = small.tile([P, 3], F32, name="mv", tag="mv", bufs=3)
+            nc.vector.bn_aggr(out=mv[:, 0:2], in_=bst[:])
+            nc.vector.tensor_scalar(
+                out=mv[:, 2:3], in0=mv[:, 0:1], scalar1=mv[:, 0:1], scalar2=mv[:, 1:2], op0=ALU.mult, op1=ALU.add
+            )
+            stt_[key] = mv
+
+        def stats_b(key):
+            ps = psum.tile([P, 4], F32, name="st", tag="st", bufs=1)
+            nc.tensor.matmul(out=ps[:, 0:3], lhsT=negg[:], rhs=stt_[key][:], start=True, stop=True)
+            stt_[key] = ps
+
+        def stats_c(key):
+            nm = small.tile([P, 3], F32, name="nm", tag="nm", bufs=4)
+            nc.vector.tensor_copy(out=nm[:], in_=stt_[key][:, 0:3])
+            nmt[key] = nm
+            t1 = small.tile([P, 1], F32, name="t1", tag="t1", bufs=3)
+            nc.gpsimd.tensor_scalar(
+                out=t1[:], in0=nm[:, 0:1], scalar1=nm[:, 0:1], scalar2=nm[:, 2:3], op0=ALU.mult, op1=ALU.add
+            )
+            u1 = small.tile([P, 1], F32, name="u1", tag="u1", bufs=3)
+            nc.gpsimd.tensor_scalar(out=u1[:], in0=t1[:], scalar1=-1.0, scalar2=EPS, op0=ALU.mult, op1=ALU.add)
+            rs = small.tile([P, 1], F32, name="rstd", tag="rstd", bufs=4)
+            nc.gpsimd.tensor_tensor(out=rs[:], in0=u1[:], in1=mhalf[:], op=ALU.pow)
+            rstd[key] = rs
+
+        def st_d1(t):
+            if ok(t):
+                stats_a(t, [acc[(t, 0)][:], acc[(t, 1)][:]])
+
+        def st_stat(t):
+            if ok(t):
+                stats_b(t)
+
+        def st_d2(t):
+            if ok(t):
+                stats_c(t)
+
+        def st_s3(t):
+            if not ok(t):
+                return
+            rz[t] = work.tile([P, C], F32, name="rz", tag="rz", bufs=4)
+            for n2 in range(2):
+                cols = slice(n2 * HALF, (n2 + 1) * HALF)
+                nc.scalar.activation(
+                    out=rz[t][:, cols], in_=acc[(t, n2)][:], func=ACTF.Relu, bias=nmt[t][:, 0:1], scale=1.0
+                )
+
+        def st_s4(t):
+            if not ok(t):
+                return
+            j, h = t // 2, t % 2
+            nc.vector.scalar_tensor_tensor(
+                out=rz[t][:],
+                in0=rz[t][:],
+                scalar=rstd[t][:, 0:1],
+                in1=ech[(h, j // 2)][:, j % 2, :],
+                op0=ALU.mult,
+                op1=ALU.add,
+            )
+            nc.sync.dma_start(out=o1[h][:, j, :], in_=rz[t][:])
+
+        def st_s56(t):
+            if not ok(t):
+                return
+            j, h = t // 2, t % 2
+            te = work.tile([P, C], F32, name="te", tag="te", bufs=3)
+            nc.scalar.activation(out=te[:], in_=rz[t][:], func=ACTF.Tanh, scale=0.5)
+            et[t] = den[h] if j == 0 else te
+            nc.scalar.activation(out=et[t][:], in_=te[:], func=ACTF.Exp, scale=0.5)
+
+        def st_ub(j):
+            if not 0 <= j < NJ:
+                return
+            for n2 in range(2):
+                u_ = psum.tile([P, HALF], F32, name="ub", tag="ub", bufs=2)
+                cols = slice(n2 * HALF, (n2 + 1) * HALF)
+                for g in range(2):
+                    mx(u_[:], xrc[:, j, g, :], xrs[:, j, g, :], wc["WV"][:, g, cols], ws["WV"][:, g, cols], g == 0, g == 1)
+                ubt[(j, n2)] = u_
+
+        def st_s7(t):
+            if not ok(t):
+                return
+            j, h = t // 2, t % 2
+            mt[t] = num[h] if j == 0 else work.tile([P, C], F32, name="mt", tag="mt", bufs=2)
+            for n2 in range(2):
+                cols = slice(n2 * HALF, (n2 + 1) * HALF)
+                nc.vector.tensor_tensor(out=mt[t][:, cols], in0=et[t][:, cols], in1=ubt[(j, n2)][:], op=ALU.mult)
+
+        def st_s8(t):
+            if not ok(t) or t < 2:
+                return
+            h = t % 2
+            nc.gpsimd.tensor_tensor(out=den[h][:], in0=den[h][:], in1=et[t][:], op=ALU.add)
+
+        def st_s9(t):
+            if not ok(t) or t < 2:
+                return
+            h = t % 2
+            eng = nc.vector
+            if S9_POOL_EVERY and t % S9_POOL_EVERY == 0:
+                eng = nc.gpsimd
+            eng.tensor_tensor(out=num[h][:], in0=num[h][:], in1=mt[t][:], op=ALU.add)
+
+        uix = {}
+        for k in range(-3, NT + 4):
+            st_d1(k - 1)
+            st_c(k, 0)
+            st_s56(k - 3)
+            st_stat(k - 1)
+            st_s8(k - 4)
+            st_s7(k - 4)
+            st_d2(k - 1)
+            st_c(k, 1)
+            st_evac(k + 2)
+            st_s3(k - 1)
+            st_s9(k - 4)
+            st_s4(k - 2)
+            st_q(k + 2)
+            if k % 2 == 1:
+                st_ub((k - 3) // 2)
+            st_tr(k + 3)
+            if k in (0, 1):
+                prep_w("WV", 2 * k, [("ub", 2)])
+                prep_w("WV", 2 * k + 1, [("ub", 2)])
+            if k in (0, 1, 2):
+                prep_xrep(k + 1)
+            if k == 2:
+                for a in range(4):
+                    load_w("WU", a)
+            if k >= 5 and (k + 7) % 4 == 0 and (k + 7) // 4 < 8:
+                load_e((k + 7) // 4)
+            if k in (NT, NT + 1):
+                prep_w("WU", 2 * (k - NT), [("acc", 4)])
+                prep_w("WU", 2 * (k - NT) + 1, [("acc", 4)])
+            if k == NT + 2:
+                for h in range(2):
+                    for n2 in range(2):
+                        u_ = psum.tile([P, HALF], F32, name="uix", tag="acc", bufs=4)
+                        cols = slice(n2 * HALF, (n2 + 1) * HALF)
+                        for g in range(2):
+                            mx(u_[:], xc[:, h, g, :], xs[:, h, g, :], wc["WU"][:, g, cols], ws["WU"][:, g, cols], g == 0, g == 1)
+                        uix[(h, n2)] = u_
+
+        xnew = {}
+        rdt = {}
+        for h in range(2):
+            rdt[h] = work.tile([P, C], F32, name="rd", tag="te", bufs=3)
+            nc.scalar.activation(out=rdt[h][:], in_=den[h][:], func=ACTF.Ln)
+        for h in range(2):
+            nc.scalar.activation(out=rdt[h][:], in_=rdt[h][:], func=ACTF.Exp, scale=-1.0)
+        for h in range(2):
+            nc.vector.tensor_tensor(out=num[h][:], in0=num[h][:], in1=rdt[h][:], op=ALU.mult)
+            xnew[h] = work.tile([P, C], F32, name="xnew", tag="rz", bufs=4)
+            for n2 in range(2):
+                cols = slice(n2 * HALF, (n2 + 1) * HALF)
+                nc.vector.scalar_tensor_tensor(
+                    out=xnew[h][:, cols],
+                    in0=num[h][:, cols],
+                    scalar=1.0 / 16.0,
+                    in1=uix[(h, n2)][:],
+                    op0=ALU.mult,
+                    op1=ALU.add,
+                )
+            stats_a(("x", h), [xnew[h][:, 0:HALF], xnew[h][:, HALF:C]])
+        for h in range(2):
+            stats_b(("x", h))
+            stats_c(("x", h))
+        for h in range(2):
+            nc.vector.tensor_scalar(
+                out=xnew[h][:],
+                in0=xnew[h][:],
+                scalar1=nmt[("x", h)][:, 0:1],
+                scalar2=rstd[("x", h)][:, 0:1],
+                op0=ALU.add,
+                op1=ALU.mult,
+            )
+            nc.vector.tensor_tensor(out=xnew[h][:], in0=xnew[h][:], in1=xn[:, h, :], op=ALU.add)
+            nc.scalar.activation(out=xnew[h][:], in_=xnew[h][:], func=ACTF.Relu)
+            nc.sync.dma_start(out=o0[h], in_=xnew[h][:])

@@ -50,6 +50,8 @@ def tile_graphmodel_pa_t_kernel(tc, x, edge, WA, WB, WE, WU, WV, out_0, out_1):
         nc.scalar.activation(out=warm2[:], in_=warm[:], func=ACTF.Exp)
         mhalf = const.tile([P, 1], F32, name="mhalf")
         nc.vector.memset(mhalf[:], -0.5)
+        epst = const.tile([P, 1], F32, name="epst")
+        nc.vector.memset(epst[:], EPS)
         ident = const.tile([P, P], F32, name="ident")
         make_identity(nc, ident[:])
         rsel = const.tile([P, 8], F32, name="rsel")
@@ -122,37 +124,43 @@ def tile_graphmodel_pa_t_kernel(tc, x, edge, WA, WB, WE, WU, WV, out_0, out_1):
         gwt = {}
 
         def prep_w(w, a, tags):
-            n2 = a // 2
             if a % 2 == 0:
-                gwt[w] = stage.tile([P, 2, 2048], BF16, name="gw", tag="gw", bufs=3, align_bytes=64)
-            gwf = gwt[w][:].bitcast(F32).rearrange("q g (r u) -> q g r u", u=2)
+                gwt[(w, a // 2)] = stage.tile([P, 2, 2048], BF16, name="gw", tag="gw", bufs=3, align_bytes=64)
+            gwf = gwt[(w, a // 2)][:].bitcast(F32).rearrange("q g (r u) -> q g r u", u=2)
             wf = wn[(w, a)][:].bitcast(F32)
             for r2 in range(2):
                 tag, bufs = tags[r2 % len(tags)]
                 bank = transposes(wf[:, r2, :], tag, bufs)
                 r0 = ((a % 2) * 2 + r2) * P
                 regroup(gwf[:, :, r0 : r0 + P, :], bank)
-            if a % 2 == 1:
-                cols = slice(n2 * HALF, (n2 + 1) * HALF)
-                for g in range(2):
-                    nc.vector.quantize_mx(
-                        out=wc[w][:, g, cols].bitcast(FP8X4),
-                        scales=ws[w][:, g, cols],
-                        in_=gwt[w][:, g, :],
-                    )
 
-        def prep_xrep(a):
-            grx = stage.tile([P, 4, 2, 512], BF16, name="grx", tag="gw", bufs=3, align_bytes=64)
-            grf = grx[:].bitcast(F32)
+        def quant_w(w, n2):
+            cols = slice(n2 * HALF, (n2 + 1) * HALF)
+            for g in range(2):
+                nc.vector.quantize_mx(
+                    out=wc[w][:, g, cols].bitcast(FP8X4),
+                    scales=ws[w][:, g, cols],
+                    in_=gwt[(w, n2)][:, g, :],
+                )
+
+        grxt = {}
+
+        def xrep_copy(a, jj, on_act):
+            if jj == 0:
+                grxt[a] = stage.tile([P, 4, 2, 512], BF16, name="grx", tag="gw", bufs=3, align_bytes=64)
+            grf = grxt[a][:].bitcast(F32)
             gxf = gx[:].bitcast(F32)
-            for jj in range(4):
-                j = 4 * a + jj
-                for g in range(2):
-                    src = gxf[:, j % 2, g, :].rearrange("q (b l u) -> q b l u", b=16, l=8)[:, :, j // 2, :]
-                    nc.vector.tensor_copy(
-                        out=grf[:, jj, g, :].rearrange("q (b i u) -> q b i u", b=16, i=8),
-                        in_=src.unsqueeze(2).to_broadcast([P, 16, 8, 2]),
-                    )
+            j = 4 * a + jj
+            for g in range(2):
+                src = gxf[:, j % 2, g, :].rearrange("q (b l u) -> q b l u", b=16, l=8)[:, :, j // 2, :]
+                dst = grf[:, jj, g, :].rearrange("q (b i u) -> q b i u", b=16, i=8)
+                if on_act:
+                    nc.scalar.copy(out=dst, in_=src.unsqueeze(2).to_broadcast([P, 16, 8, 2]))
+                else:
+                    nc.vector.tensor_copy(out=dst, in_=src.unsqueeze(2).to_broadcast([P, 16, 8, 2]))
+
+        def xrep_quant(a):
+            grx = grxt[a]
             nc.vector.quantize_mx(
                 out=xrc[:, 4 * a : 4 * a + 4, :, :].rearrange("q j g r -> q (j g r)").bitcast(FP8X4),
                 scales=xrs[:, 4 * a : 4 * a + 4, :, :].rearrange("q j g r -> q (j g r)"),
@@ -175,9 +183,12 @@ def tile_graphmodel_pa_t_kernel(tc, x, edge, WA, WB, WE, WU, WV, out_0, out_1):
                         scales=xs[:].rearrange("q h g r -> q (h g r)"),
                         in_=gx[:].rearrange("q h g w -> q (h g w)"),
                     )
-                    prep_xrep(0)
+                    for jj in range(4):
+                        xrep_copy(0, jj, False)
+                    xrep_quant(0)
                 prep_w(w, 2 * n2, start_tags)
                 prep_w(w, 2 * n2 + 1, start_tags)
+                quant_w(w, n2)
         load_e(1)
         for a in range(4):
             load_w("WV", a)
@@ -242,14 +253,19 @@ def tile_graphmodel_pa_t_kernel(tc, x, edge, WA, WB, WE, WU, WV, out_0, out_1):
                     mx(a_[:], lc[:, g, :], ls[:, g, :], wc[w][:, g, cols], ws[w][:, g, cols], i == 0, i == 5)
                     i += 1
 
-        def stats_a(key, srcs):
-            bst = small.tile([P, 12], F32, name="bst", tag="bst", bufs=3)
-            for n2 in range(2):
-                nc.vector.bn_stats(out=bst[:, 6 * n2 : 6 * n2 + 6], in_=srcs[n2])
+        bstt = {}
+
+        def stats_a1(key, n2, src):
+            if n2 == 0:
+                bstt[key] = small.tile([P, 12], F32, name="bst", tag="bst", bufs=3)
+            nc.vector.bn_stats(out=bstt[key][:, 6 * n2 : 6 * n2 + 6], in_=src)
+
+        def stats_a2(key):
+            bst = bstt[key]
             mv = small.tile([P, 3], F32, name="mv", tag="mv", bufs=3)
             nc.vector.bn_aggr(out=mv[:, 0:2], in_=bst[:])
-            nc.vector.tensor_scalar(
-                out=mv[:, 2:3], in0=mv[:, 0:1], scalar1=mv[:, 0:1], scalar2=mv[:, 1:2], op0=ALU.mult, op1=ALU.add
+            nc.scalar.activation(
+                out=mv[:, 2:3], in_=mv[:, 0:1], func=ACTF.Identity, scale=mv[:, 0:1], bias=mv[:, 1:2]
             )
             stt_[key] = mv
 
@@ -260,21 +276,21 @@ def tile_graphmodel_pa_t_kernel(tc, x, edge, WA, WB, WE, WU, WV, out_0, out_1):
 
         def stats_c(key):
             nm = small.tile([P, 3], F32, name="nm", tag="nm", bufs=4)
-            nc.vector.tensor_copy(out=nm[:], in_=stt_[key][:, 0:3])
+            nc.scalar.copy(out=nm[:], in_=stt_[key][:, 0:3])
             nmt[key] = nm
             t1 = small.tile([P, 1], F32, name="t1", tag="t1", bufs=3)
-            nc.gpsimd.tensor_scalar(
-                out=t1[:], in0=nm[:, 0:1], scalar1=nm[:, 0:1], scalar2=nm[:, 2:3], op0=ALU.mult, op1=ALU.add
-            )
+            nc.scalar.activation(out=t1[:], in_=nm[:, 0:1], func=ACTF.Identity, scale=nm[:, 0:1], bias=nm[:, 2:3])
             u1 = small.tile([P, 1], F32, name="u1", tag="u1", bufs=3)
-            nc.gpsimd.tensor_scalar(out=u1[:], in0=t1[:], scalar1=-1.0, scalar2=EPS, op0=ALU.mult, op1=ALU.add)
+            nc.scalar.activation(out=u1[:], in_=t1[:], func=ACTF.Identity, scale=-1.0, bias=epst[:, 0:1])
             rs = small.tile([P, 1], F32, name="rstd", tag="rstd", bufs=4)
             nc.gpsimd.tensor_tensor(out=rs[:], in0=u1[:], in1=mhalf[:], op=ALU.pow)
             rstd[key] = rs
 
         def st_d1(t):
             if ok(t):
-                stats_a(t, [acc[(t, 0)][:], acc[(t, 1)][:]])
+                stats_a1(t, 0, acc[(t, 0)][:])
+                stats_a1(t, 1, acc[(t, 1)][:])
+                stats_a2(t)
 
         def st_stat(t):
             if ok(t):
@@ -340,7 +356,8 @@ def tile_graphmodel_pa_t_kernel(tc, x, edge, WA, WB, WE, WU, WV, out_0, out_1):
             if not ok(t) or t < 2:
                 return
             h = t % 2
-            nc.gpsimd.tensor_tensor(out=den[h][:], in0=den[h][:], in1=et[t][:], op=ALU.add)
+            eng = nc.vector if t >= NT - 2 else nc.gpsimd
+            eng.tensor_tensor(out=den[h][:], in0=den[h][:], in1=et[t][:], op=ALU.add)
 
         def st_s9(t):
             if not ok(t) or t < 2:
@@ -352,78 +369,97 @@ def tile_graphmodel_pa_t_kernel(tc, x, edge, WA, WB, WE, WU, WV, out_0, out_1):
             eng.tensor_tensor(out=num[h][:], in0=num[h][:], in1=mt[t][:], op=ALU.add)
 
         uix = {}
-        for k in range(-3, NT + 4):
+
+        def st_uix():
+            for h in range(2):
+                for n2 in range(2):
+                    u_ = psum.tile([P, HALF], F32, name="uix", tag="acc", bufs=4)
+                    cols = slice(n2 * HALF, (n2 + 1) * HALF)
+                    for g in range(2):
+                        mx(u_[:], xc[:, h, g, :], xs[:, h, g, :], wc["WU"][:, g, cols], ws["WU"][:, g, cols], g == 0, g == 1)
+                    uix[(h, n2)] = u_
+
+        late_p = {0: [("WV", 0), ("WV", 1)], 1: [("WV", 2), ("WV", 3)], NT - 1: [("WU", 0)], NT: [("WU", 1), ("WU", 2)], NT + 1: [("WU", 3)]}
+        late_q = {1: ("WV", 0), 2: ("WV", 1), NT + 1: ("WU", 0), NT + 2: ("WU", 1)}
+        for k in range(-3, NT + 3):
             st_d1(k - 1)
             st_c(k, 0)
-            st_s56(k - 3)
+            st_evac(k + 2)
+            st_s8(k - 3)
             st_stat(k - 1)
-            st_s8(k - 4)
-            st_s7(k - 4)
+            st_s7(k - 3)
             st_d2(k - 1)
             st_c(k, 1)
-            st_evac(k + 2)
             st_s3(k - 1)
-            st_s9(k - 4)
-            st_s4(k - 2)
+            st_s9(k - 3)
+            if k in late_q:
+                quant_w(late_q[k][0], late_q[k][1])
+            st_s4(k - 1)
+            st_s56(k - 2)
+            if k - 2 == NT - 1:
+                nc.scalar.activation(out=warm2[:], in_=epst[:], func=ACTF.Ln)
             st_q(k + 2)
-            if k % 2 == 1:
-                st_ub((k - 3) // 2)
+            if k % 2 == 0:
+                st_ub((k - 2) // 2)
             st_tr(k + 3)
-            if k in (0, 1):
-                prep_w("WV", 2 * k, [("ub", 2)])
-                prep_w("WV", 2 * k + 1, [("ub", 2)])
-            if k in (0, 1, 2):
-                prep_xrep(k + 1)
-            if k == 2:
+            for a in (1, 2, 3):
+                if 8 * a - 7 <= k <= 8 * a - 4:
+                    xrep_copy(a, k - (8 * a - 7), True)
+                if k == 8 * a - 3:
+                    xrep_quant(a)
+            for w, a in late_p.get(k, []):
+                prep_w(w, a, [("ub", 2)] if k < 2 else [("acc", 4)])
+            if k == 1:
                 for a in range(4):
                     load_w("WU", a)
-            if k >= 5 and (k + 7) % 4 == 0 and (k + 7) // 4 < 8:
-                load_e((k + 7) // 4)
-            if k in (NT, NT + 1):
-                prep_w("WU", 2 * (k - NT), [("acc", 4)])
-                prep_w("WU", 2 * (k - NT) + 1, [("acc", 4)])
+            if k >= 4 and k % 4 == 0 and k // 4 + 2 < 8:
+                load_e(k // 4 + 2)
             if k == NT + 2:
-                for h in range(2):
-                    for n2 in range(2):
-                        u_ = psum.tile([P, HALF], F32, name="uix", tag="acc", bufs=4)
-                        cols = slice(n2 * HALF, (n2 + 1) * HALF)
-                        for g in range(2):
-                            mx(u_[:], xc[:, h, g, :], xs[:, h, g, :], wc["WU"][:, g, cols], ws["WU"][:, g, cols], g == 0, g == 1)
-                        uix[(h, n2)] = u_
+                st_uix()
 
+        units = [(h, n2) for h in range(2) for n2 in range(2)]
         xnew = {}
         rdt = {}
         for h in range(2):
             rdt[h] = work.tile([P, C], F32, name="rd", tag="te", bufs=3)
-            nc.scalar.activation(out=rdt[h][:], in_=den[h][:], func=ACTF.Ln)
-        for h in range(2):
-            nc.scalar.activation(out=rdt[h][:], in_=rdt[h][:], func=ACTF.Exp, scale=-1.0)
-        for h in range(2):
-            nc.vector.tensor_tensor(out=num[h][:], in0=num[h][:], in1=rdt[h][:], op=ALU.mult)
             xnew[h] = work.tile([P, C], F32, name="xnew", tag="rz", bufs=4)
+        for h, n2 in units:
+            cols = slice(n2 * HALF, (n2 + 1) * HALF)
+            nc.scalar.activation(out=rdt[h][:, cols], in_=den[h][:, cols], func=ACTF.Ln)
+        for h, n2 in units:
+            cols = slice(n2 * HALF, (n2 + 1) * HALF)
+            nc.scalar.activation(out=rdt[h][:, cols], in_=rdt[h][:, cols], func=ACTF.Exp, scale=-1.0)
+        for h, n2 in units:
+            cols = slice(n2 * HALF, (n2 + 1) * HALF)
+            nc.vector.tensor_tensor(out=num[h][:, cols], in0=num[h][:, cols], in1=rdt[h][:, cols], op=ALU.mult)
+            nc.vector.scalar_tensor_tensor(
+                out=xnew[h][:, cols],
+                in0=num[h][:, cols],
+                scalar=1.0 / 16.0,
+                in1=uix[(h, n2)][:],
+                op0=ALU.mult,
+                op1=ALU.add,
+            )
+            stats_a1(("x", h), n2, xnew[h][:, cols])
+            if n2 == 1:
+                stats_a2(("x", h))
+                stats_b(("x", h))
+                stats_c(("x", h))
+        for h in range(2):
+            key = ("x", h)
+            nb = small.tile([P, 1], F32, name="nb", tag="nb", bufs=2)
+            nc.gpsimd.tensor_tensor(out=nb[:], in0=nmt[key][:, 0:1], in1=rstd[key][:], op=ALU.mult)
             for n2 in range(2):
                 cols = slice(n2 * HALF, (n2 + 1) * HALF)
                 nc.vector.scalar_tensor_tensor(
                     out=xnew[h][:, cols],
-                    in0=num[h][:, cols],
-                    scalar=1.0 / 16.0,
-                    in1=uix[(h, n2)][:],
+                    in0=xnew[h][:, cols],
+                    scalar=rstd[key][:, 0:1],
+                    in1=xn[:, h, cols],
                     op0=ALU.mult,
                     op1=ALU.add,
                 )
-            stats_a(("x", h), [xnew[h][:, 0:HALF], xnew[h][:, HALF:C]])
-        for h in range(2):
-            stats_b(("x", h))
-            stats_c(("x", h))
-        for h in range(2):
-            nc.vector.tensor_scalar(
-                out=xnew[h][:],
-                in0=xnew[h][:],
-                scalar1=nmt[("x", h)][:, 0:1],
-                scalar2=rstd[("x", h)][:, 0:1],
-                op0=ALU.add,
-                op1=ALU.mult,
-            )
-            nc.vector.tensor_tensor(out=xnew[h][:], in0=xnew[h][:], in1=xn[:, h, :], op=ALU.add)
-            nc.scalar.activation(out=xnew[h][:], in_=xnew[h][:], func=ACTF.Relu)
+                nc.scalar.activation(
+                    out=xnew[h][:, cols], in_=xnew[h][:, cols], func=ACTF.Relu, bias=nb[:, 0:1], scale=1.0
+                )
             nc.sync.dma_start(out=o0[h], in_=xnew[h][:])

@@ -20,7 +20,7 @@ HALF = 512
 EPS = 1e-5
 FLOPS = 2 * 1024 * 1024 * (4096 + 4 * 256)
 
-PIN = True
+PIN = False
 S9_POOL_EVERY = 0
 
 

@@ -20,8 +20,17 @@ HALF = 512
 EPS = 1e-5
 FLOPS = 2 * 1024 * 1024 * (4096 + 4 * 256)
 
-PIN = False
+PIN = True
 S9_POOL_EVERY = 0
+S8_ON_DVE = False
+RZ_BUFS = 5
+TE_BUFS = 3
+MT_BUFS = 2
+WU_K0 = 8
+EPI = True
+SCHED = [
+    ("s6", 4), ("evac", -2), ("c0", 0), ("bn0", 0), ("s8", 4), ("stat", 1), ("s7a", 4), ("s7b", 4), ("nm", 1), ("c1", 0), ("s3a", 1), ("s3b", 1), ("chain", 1), ("bn1", 0), ("aggr", 0), ("e2", 0), ("lateq", 0), ("s4", 2), ("q", -2), ("s9", 4), ("s5", 3), ("ub", 3), ("wut", 0), ("tr", -3), ("wur", 0),
+]
 
 
 def tile_graphmodel_pa_t_kernel(tc, x, edge, WA, WB, WE, WU, WV, out_0, out_1):
@@ -123,16 +132,26 @@ def tile_graphmodel_pa_t_kernel(tc, x, edge, WA, WB, WE, WU, WV, out_0, out_1):
 
         gwt = {}
 
+        ubank = {}
+
+        def unit_t(w, a, r2, tag, bufs):
+            ubank[(w, a, r2)] = transposes(wn[(w, a)][:].bitcast(F32)[:, r2, :], tag, bufs)
+
+        def unit_r(w, a, r2):
+            gwf = gwt[(w, a // 2)][:].bitcast(F32).rearrange("q g (r u) -> q g r u", u=2)
+            r0 = ((a % 2) * 2 + r2) * P
+            regroup(gwf[:, :, r0 : r0 + P, :], ubank[(w, a, r2)])
+
+        def new_gw(w, n2):
+            gwt[(w, n2)] = stage.tile([P, 2, 2048], BF16, name="gw", tag="gw", bufs=3, align_bytes=64)
+
         def prep_w(w, a, tags):
             if a % 2 == 0:
-                gwt[(w, a // 2)] = stage.tile([P, 2, 2048], BF16, name="gw", tag="gw", bufs=3, align_bytes=64)
-            gwf = gwt[(w, a // 2)][:].bitcast(F32).rearrange("q g (r u) -> q g r u", u=2)
-            wf = wn[(w, a)][:].bitcast(F32)
+                new_gw(w, a // 2)
             for r2 in range(2):
                 tag, bufs = tags[r2 % len(tags)]
-                bank = transposes(wf[:, r2, :], tag, bufs)
-                r0 = ((a % 2) * 2 + r2) * P
-                regroup(gwf[:, :, r0 : r0 + P, :], bank)
+                unit_t(w, a, r2, tag, bufs)
+                unit_r(w, a, r2)
 
         def quant_w(w, n2):
             cols = slice(n2 * HALF, (n2 + 1) * HALF)
@@ -167,33 +186,6 @@ def tile_graphmodel_pa_t_kernel(tc, x, edge, WA, WB, WE, WU, WV, out_0, out_1):
                 in_=grx[:].rearrange("q j g w -> q (j g w)"),
             )
 
-        start_tags = [("acc", 4), ("ub", 2)]
-        for n2 in range(2):
-            for w in ("WE", "WA", "WB"):
-                load_w(w, 2 * n2)
-                load_w(w, 2 * n2 + 1)
-                if n2 == 0 and w == "WE":
-                    gxf0 = gx[:].bitcast(F32)
-                    xf = xn[:].bitcast(F32)
-                    for h in range(2):
-                        bank = transposes(xf[:, h, :], "acc", 4)
-                        regroup(gxf0[:, h, :, :].rearrange("q g (r u) -> q g r u", u=2), bank)
-                    nc.vector.quantize_mx(
-                        out=xc[:].rearrange("q h g r -> q (h g r)").bitcast(FP8X4),
-                        scales=xs[:].rearrange("q h g r -> q (h g r)"),
-                        in_=gx[:].rearrange("q h g w -> q (h g w)"),
-                    )
-                    for jj in range(4):
-                        xrep_copy(0, jj, False)
-                    xrep_quant(0)
-                prep_w(w, 2 * n2, start_tags)
-                prep_w(w, 2 * n2 + 1, start_tags)
-                quant_w(w, n2)
-        load_e(1)
-        for a in range(4):
-            load_w("WV", a)
-        load_e(2)
-
         ge = {}
         ecs = {}
         trb = {}
@@ -209,12 +201,12 @@ def tile_graphmodel_pa_t_kernel(tc, x, edge, WA, WB, WE, WU, WV, out_0, out_1):
         def ok(t):
             return 0 <= t < NT
 
-        def st_tr(t):
+        def st_tr(t, tag="tr", bufs=1):
             if not ok(t):
                 return
             j, h = t // 2, t % 2
             ef = ech[(h, j // 2)][:].bitcast(F32)
-            trb[t] = transposes(ef[:, j % 2, :], "tr", 1)
+            trb[t] = transposes(ef[:, j % 2, :], tag, bufs)
 
         def st_evac(t):
             if not ok(t):
@@ -261,16 +253,18 @@ def tile_graphmodel_pa_t_kernel(tc, x, edge, WA, WB, WE, WU, WV, out_0, out_1):
             nc.vector.bn_stats(out=bstt[key][:, 6 * n2 : 6 * n2 + 6], in_=src)
 
         def stats_a2(key):
-            bst = bstt[key]
             mv = small.tile([P, 3], F32, name="mv", tag="mv", bufs=3)
-            nc.vector.bn_aggr(out=mv[:, 0:2], in_=bst[:])
-            nc.scalar.activation(
-                out=mv[:, 2:3], in_=mv[:, 0:1], func=ACTF.Identity, scale=mv[:, 0:1], bias=mv[:, 1:2]
-            )
+            nc.vector.bn_aggr(out=mv[:, 0:2], in_=bstt[key][:])
             stt_[key] = mv
 
+        def stats_a3(key):
+            mv = stt_[key]
+            nc.vector.tensor_scalar(
+                out=mv[:, 2:3], in0=mv[:, 0:1], scalar1=mv[:, 0:1], scalar2=mv[:, 1:2], op0=ALU.mult, op1=ALU.add
+            )
+
         def stats_b(key):
-            ps = psum.tile([P, 4], F32, name="st", tag="st", bufs=1)
+            ps = psum.tile([P, HALF], F32, name="st", tag="st", bufs=1)
             nc.tensor.matmul(out=ps[:, 0:3], lhsT=negg[:], rhs=stt_[key][:], start=True, stop=True)
             stt_[key] = ps
 
@@ -278,6 +272,11 @@ def tile_graphmodel_pa_t_kernel(tc, x, edge, WA, WB, WE, WU, WV, out_0, out_1):
             nm = small.tile([P, 3], F32, name="nm", tag="nm", bufs=4)
             nc.scalar.copy(out=nm[:], in_=stt_[key][:, 0:3])
             nmt[key] = nm
+
+        nbt = {}
+
+        def stats_d(key, want_nb=False):
+            nm = nmt[key]
             t1 = small.tile([P, 1], F32, name="t1", tag="t1", bufs=3)
             nc.scalar.activation(out=t1[:], in_=nm[:, 0:1], func=ACTF.Identity, scale=nm[:, 0:1], bias=nm[:, 2:3])
             u1 = small.tile([P, 1], F32, name="u1", tag="u1", bufs=3)
@@ -285,30 +284,44 @@ def tile_graphmodel_pa_t_kernel(tc, x, edge, WA, WB, WE, WU, WV, out_0, out_1):
             rs = small.tile([P, 1], F32, name="rstd", tag="rstd", bufs=4)
             nc.gpsimd.tensor_tensor(out=rs[:], in0=u1[:], in1=mhalf[:], op=ALU.pow)
             rstd[key] = rs
+            if want_nb:
+                nb = small.tile([P, 1], F32, name="nb", tag="nb", bufs=2)
+                nc.gpsimd.tensor_tensor(out=nb[:], in0=nm[:, 0:1], in1=rs[:], op=ALU.mult)
+                nbt[key] = nb
 
-        def st_d1(t):
+        def st_bn(t, n2):
             if ok(t):
-                stats_a1(t, 0, acc[(t, 0)][:])
-                stats_a1(t, 1, acc[(t, 1)][:])
+                stats_a1(t, n2, acc[(t, n2)][:])
+
+        def st_aggr(t):
+            if ok(t):
                 stats_a2(t)
+
+        def st_e2(t):
+            if ok(t):
+                stats_a3(t)
 
         def st_stat(t):
             if ok(t):
                 stats_b(t)
 
-        def st_d2(t):
+        def st_nm(t):
             if ok(t):
                 stats_c(t)
 
-        def st_s3(t):
+        def st_chain(t):
+            if ok(t):
+                stats_d(t)
+
+        def st_s3(t, n2):
             if not ok(t):
                 return
-            rz[t] = work.tile([P, C], F32, name="rz", tag="rz", bufs=4)
-            for n2 in range(2):
-                cols = slice(n2 * HALF, (n2 + 1) * HALF)
-                nc.scalar.activation(
-                    out=rz[t][:, cols], in_=acc[(t, n2)][:], func=ACTF.Relu, bias=nmt[t][:, 0:1], scale=1.0
-                )
+            if n2 == 0:
+                rz[t] = work.tile([P, C], F32, name="rz", tag="rz", bufs=RZ_BUFS)
+            cols = slice(n2 * HALF, (n2 + 1) * HALF)
+            nc.scalar.activation(
+                out=rz[t][:, cols], in_=acc[(t, n2)][:], func=ACTF.Relu, bias=nmt[t][:, 0:1], scale=1.0
+            )
 
         def st_s4(t):
             if not ok(t):
@@ -324,14 +337,22 @@ def tile_graphmodel_pa_t_kernel(tc, x, edge, WA, WB, WE, WU, WV, out_0, out_1):
             )
             nc.sync.dma_start(out=o1[h][:, j, :], in_=rz[t][:])
 
-        def st_s56(t):
+        tet = {}
+
+        def st_s5(t):
+            if not ok(t):
+                return
+            tet[t] = work.tile([P, C], F32, name="te", tag="te", bufs=TE_BUFS)
+            nc.scalar.activation(out=tet[t][:], in_=rz[t][:], func=ACTF.Tanh, scale=0.5)
+
+        def st_s6(t):
             if not ok(t):
                 return
             j, h = t // 2, t % 2
-            te = work.tile([P, C], F32, name="te", tag="te", bufs=3)
-            nc.scalar.activation(out=te[:], in_=rz[t][:], func=ACTF.Tanh, scale=0.5)
-            et[t] = den[h] if j == 0 else te
-            nc.scalar.activation(out=et[t][:], in_=te[:], func=ACTF.Exp, scale=0.5)
+            et[t] = den[h] if j == 0 else tet[t]
+            nc.scalar.activation(out=et[t][:], in_=tet[t][:], func=ACTF.Exp, scale=0.5)
+            if t == NT - 1:
+                nc.scalar.activation(out=warm2[:], in_=epst[:], func=ACTF.Ln)
 
         def st_ub(j):
             if not 0 <= j < NJ:
@@ -343,20 +364,20 @@ def tile_graphmodel_pa_t_kernel(tc, x, edge, WA, WB, WE, WU, WV, out_0, out_1):
                     mx(u_[:], xrc[:, j, g, :], xrs[:, j, g, :], wc["WV"][:, g, cols], ws["WV"][:, g, cols], g == 0, g == 1)
                 ubt[(j, n2)] = u_
 
-        def st_s7(t):
+        def st_s7(t, n2):
             if not ok(t):
                 return
             j, h = t // 2, t % 2
-            mt[t] = num[h] if j == 0 else work.tile([P, C], F32, name="mt", tag="mt", bufs=2)
-            for n2 in range(2):
-                cols = slice(n2 * HALF, (n2 + 1) * HALF)
-                nc.vector.tensor_tensor(out=mt[t][:, cols], in0=et[t][:, cols], in1=ubt[(j, n2)][:], op=ALU.mult)
+            if n2 == 0:
+                mt[t] = num[h] if j == 0 else work.tile([P, C], F32, name="mt", tag="mt", bufs=MT_BUFS)
+            cols = slice(n2 * HALF, (n2 + 1) * HALF)
+            nc.vector.tensor_tensor(out=mt[t][:, cols], in0=et[t][:, cols], in1=ubt[(j, n2)][:], op=ALU.mult)
 
         def st_s8(t):
             if not ok(t) or t < 2:
                 return
             h = t % 2
-            eng = nc.vector if t >= NT - 2 else nc.gpsimd
+            eng = nc.vector if (t >= NT - 4 or S8_ON_DVE) else nc.gpsimd
             eng.tensor_tensor(out=den[h][:], in0=den[h][:], in1=et[t][:], op=ALU.add)
 
         def st_s9(t):
@@ -367,6 +388,39 @@ def tile_graphmodel_pa_t_kernel(tc, x, edge, WA, WB, WE, WU, WV, out_0, out_1):
             if S9_POOL_EVERY and t % S9_POOL_EVERY == 0:
                 eng = nc.gpsimd
             eng.tensor_tensor(out=num[h][:], in0=num[h][:], in1=mt[t][:], op=ALU.add)
+
+        start_tags = [("acc", 4), ("ub", 2)]
+        for n2 in range(2):
+            for w in ("WE", "WA", "WB"):
+                load_w(w, 2 * n2)
+                load_w(w, 2 * n2 + 1)
+                if n2 == 0 and w == "WE":
+                    gxf0 = gx[:].bitcast(F32)
+                    xf = xn[:].bitcast(F32)
+                    for h in range(2):
+                        bank = transposes(xf[:, h, :], "acc", 4)
+                        regroup(gxf0[:, h, :, :].rearrange("q g (r u) -> q g r u", u=2), bank)
+                    nc.vector.quantize_mx(
+                        out=xc[:].rearrange("q h g r -> q (h g r)").bitcast(FP8X4),
+                        scales=xs[:].rearrange("q h g r -> q (h g r)"),
+                        in_=gx[:].rearrange("q h g w -> q (h g w)"),
+                    )
+                    for t in range(2):
+                        st_tr(t, "acc", 4)
+                        st_evac(t)
+                    for jj in range(4):
+                        xrep_copy(0, jj, False)
+                    for t in range(2):
+                        st_q(t)
+                    xrep_quant(0)
+                    st_tr(2)
+                prep_w(w, 2 * n2, start_tags)
+                prep_w(w, 2 * n2 + 1, start_tags)
+                quant_w(w, n2)
+        load_e(1)
+        for a in range(4):
+            load_w("WV", a)
+        load_e(2)
 
         uix = {}
 
@@ -379,29 +433,60 @@ def tile_graphmodel_pa_t_kernel(tc, x, edge, WA, WB, WE, WU, WV, out_0, out_1):
                         mx(u_[:], xc[:, h, g, :], xs[:, h, g, :], wc["WU"][:, g, cols], ws["WU"][:, g, cols], g == 0, g == 1)
                     uix[(h, n2)] = u_
 
-        late_p = {0: [("WV", 0), ("WV", 1)], 1: [("WV", 2), ("WV", 3)], NT - 1: [("WU", 0)], NT: [("WU", 1), ("WU", 2)], NT + 1: [("WU", 3)]}
-        late_q = {1: ("WV", 0), 2: ("WV", 1), NT + 1: ("WU", 0), NT + 2: ("WU", 1)}
-        for k in range(-3, NT + 3):
-            st_d1(k - 1)
-            st_c(k, 0)
-            st_evac(k + 2)
-            st_s8(k - 3)
-            st_stat(k - 1)
-            st_s7(k - 3)
-            st_d2(k - 1)
-            st_c(k, 1)
-            st_s3(k - 1)
-            st_s9(k - 3)
-            if k in late_q:
-                quant_w(late_q[k][0], late_q[k][1])
-            st_s4(k - 1)
-            st_s56(k - 2)
-            if k - 2 == NT - 1:
-                nc.scalar.activation(out=warm2[:], in_=epst[:], func=ACTF.Ln)
-            st_q(k + 2)
-            if k % 2 == 0:
-                st_ub((k - 2) // 2)
-            st_tr(k + 3)
+        late_p = {0: [("WV", 0), ("WV", 1)], 1: [("WV", 2), ("WV", 3)]}
+        late_q = {1: ("WV", 0), 2: ("WV", 1), WU_K0 + 8: ("WU", 0), WU_K0 + 16: ("WU", 1)}
+
+        def wu_unit(k):
+            u = (k - WU_K0) // 2
+            if (k - WU_K0) % 2 != 0 or not 0 <= u < 8:
+                return None
+            return ("WU", u // 2, u % 2)
+
+        stages = {
+            "c0": lambda t: st_c(t, 0),
+            "c1": lambda t: st_c(t, 1),
+            "bn0": lambda t: st_bn(t, 0),
+            "bn1": lambda t: st_bn(t, 1),
+            "aggr": st_aggr,
+            "e2": st_e2,
+            "stat": st_stat,
+            "nm": st_nm,
+            "chain": st_chain,
+            "s3a": lambda t: st_s3(t, 0),
+            "s3b": lambda t: st_s3(t, 1),
+            "s4": st_s4,
+            "s5": st_s5,
+            "s6": st_s6,
+            "s7a": lambda t: st_s7(t, 0),
+            "s7b": lambda t: st_s7(t, 1),
+            "s8": st_s8,
+            "s9": st_s9,
+            "q": st_q,
+            "evac": st_evac,
+            "tr": st_tr,
+        }
+        last = max(lag for name, lag in SCHED)
+        s4lag = dict(SCHED)["s4"]
+        for k in range(0, NT if EPI else NT + last + 1):
+            for name, lag in SCHED:
+                if name == "ub":
+                    if (k - lag) % 2 == 0:
+                        st_ub((k - lag) // 2)
+                elif name == "wut":
+                    un = wu_unit(k)
+                    if un is not None:
+                        if un[1] % 2 == 0 and un[2] == 0:
+                            new_gw("WU", un[1] // 2)
+                        unit_t(un[0], un[1], un[2], "st", 1)
+                elif name == "wur":
+                    un = wu_unit(k)
+                    if un is not None:
+                        unit_r(un[0], un[1], un[2])
+                elif name == "lateq":
+                    if k in late_q:
+                        quant_w(late_q[k][0], late_q[k][1])
+                else:
+                    stages[name](k - lag)
             for a in (1, 2, 3):
                 if 8 * a - 7 <= k <= 8 * a - 4:
                     xrep_copy(a, k - (8 * a - 7), True)
@@ -412,26 +497,58 @@ def tile_graphmodel_pa_t_kernel(tc, x, edge, WA, WB, WE, WU, WV, out_0, out_1):
             if k == 1:
                 for a in range(4):
                     load_w("WU", a)
-            if k >= 4 and k % 4 == 0 and k // 4 + 2 < 8:
-                load_e(k // 4 + 2)
+            if k >= 3 and (k + 9 - s4lag) % 4 == 0 and 3 <= (k + 9 - s4lag) // 4 < 8:
+                load_e((k + 9 - s4lag) // 4)
             if k == NT + 2:
                 st_uix()
+        if EPI:
+            st_s6(NT - 4)
+            st_stat(NT - 1)
+            st_s4(NT - 2)
+            st_s5(NT - 3)
+            st_nm(NT - 1)
+            st_s3(NT - 1, 0)
+            st_s3(NT - 1, 1)
+            st_chain(NT - 1)
+            for t in (NT - 4, NT - 3):
+                st_s8(t)
+                st_s7(t, 0)
+                st_s7(t, 1)
+                st_s6(t + 1)
+                st_s9(t)
+                st_s5(t + 2)
+                if t == NT - 4:
+                    st_s4(NT - 1)
+            st_ub(NJ - 1)
+            st_uix()
+            st_s8(NT - 2)
+            st_s6(NT - 1)
+            st_s7(NT - 2, 0)
+            st_s7(NT - 2, 1)
+            st_s8(NT - 1)
+            st_s9(NT - 2)
+            st_s7(NT - 1, 0)
+            st_s7(NT - 1, 1)
+            st_s9(NT - 1)
 
         units = [(h, n2) for h in range(2) for n2 in range(2)]
         xnew = {}
         rdt = {}
         for h in range(2):
-            rdt[h] = work.tile([P, C], F32, name="rd", tag="te", bufs=3)
-            xnew[h] = work.tile([P, C], F32, name="xnew", tag="rz", bufs=4)
+            rdt[h] = work.tile([P, C], F32, name="rd", tag="te", bufs=TE_BUFS)
+            xnew[h] = work.tile([P, C], F32, name="xnew", tag="rz", bufs=RZ_BUFS)
         for h, n2 in units:
             cols = slice(n2 * HALF, (n2 + 1) * HALF)
             nc.scalar.activation(out=rdt[h][:, cols], in_=den[h][:, cols], func=ACTF.Ln)
         for h, n2 in units:
             cols = slice(n2 * HALF, (n2 + 1) * HALF)
             nc.scalar.activation(out=rdt[h][:, cols], in_=rdt[h][:, cols], func=ACTF.Exp, scale=-1.0)
-        for h, n2 in units:
+        def tail_mul(h, n2):
             cols = slice(n2 * HALF, (n2 + 1) * HALF)
             nc.vector.tensor_tensor(out=num[h][:, cols], in0=num[h][:, cols], in1=rdt[h][:, cols], op=ALU.mult)
+
+        def tail_add(h, n2):
+            cols = slice(n2 * HALF, (n2 + 1) * HALF)
             nc.vector.scalar_tensor_tensor(
                 out=xnew[h][:, cols],
                 in0=num[h][:, cols],
@@ -440,15 +557,32 @@ def tile_graphmodel_pa_t_kernel(tc, x, edge, WA, WB, WE, WU, WV, out_0, out_1):
                 op0=ALU.mult,
                 op1=ALU.add,
             )
+
+        def tail_bn(h, n2):
+            cols = slice(n2 * HALF, (n2 + 1) * HALF)
             stats_a1(("x", h), n2, xnew[h][:, cols])
-            if n2 == 1:
-                stats_a2(("x", h))
-                stats_b(("x", h))
-                stats_c(("x", h))
+
+        for f in (tail_mul, tail_add, tail_bn):
+            f(0, 0)
+            f(0, 1)
+        tail_mul(1, 0)
+        stats_a2(("x", 0))
+        tail_mul(1, 1)
+        stats_a3(("x", 0))
+        stats_b(("x", 0))
+        stats_c(("x", 0))
+        stats_d(("x", 0), True)
+        for f in (tail_add, tail_bn):
+            f(1, 0)
+            f(1, 1)
+        stats_a2(("x", 1))
+        stats_a3(("x", 1))
+        stats_b(("x", 1))
+        stats_c(("x", 1))
+        stats_d(("x", 1), True)
         for h in range(2):
             key = ("x", h)
-            nb = small.tile([P, 1], F32, name="nb", tag="nb", bufs=2)
-            nc.gpsimd.tensor_tensor(out=nb[:], in0=nmt[key][:, 0:1], in1=rstd[key][:], op=ALU.mult)
+            nb = nbt[key]
             for n2 in range(2):
                 cols = slice(n2 * HALF, (n2 + 1) * HALF)
                 nc.vector.scalar_tensor_tensor(
@@ -462,4 +596,4 @@ def tile_graphmodel_pa_t_kernel(tc, x, edge, WA, WB, WE, WU, WV, out_0, out_1):
                 nc.scalar.activation(
                     out=xnew[h][:, cols], in_=xnew[h][:, cols], func=ACTF.Relu, bias=nb[:, 0:1], scale=1.0
                 )
-            nc.sync.dma_start(out=o0[h], in_=xnew[h][:])
+                nc.sync.dma_start(out=o0[h][:, cols], in_=xnew[h][:, cols])

@@ -27,9 +27,12 @@ RZ_BUFS = 5
 TE_BUFS = 3
 MT_BUFS = 2
 WU_K0 = 8
+WV_UNITS = {0: [0, 1, 2, 3], 1: [4, 5, 6, 7]}
+WV_Q = (1, 2)
 EPI = True
+TAIL_POOL = True
 SCHED = [
-    ("s6", 4), ("evac", -2), ("c0", 0), ("bn0", 0), ("s8", 4), ("stat", 1), ("s7a", 4), ("s7b", 4), ("nm", 1), ("c1", 0), ("s3a", 1), ("s3b", 1), ("chain", 1), ("bn1", 0), ("aggr", 0), ("e2", 0), ("lateq", 0), ("s4", 2), ("q", -2), ("s9", 4), ("s5", 3), ("ub", 3), ("wut", 0), ("tr", -3), ("wur", 0),
+    ("s6", 4), ("evac", -2), ("c0", 0), ("bn0", 0), ("stat", 1), ("s7a", 4), ("s8", 4), ("nm", 1), ("s3a", 1), ("c1", 0), ("s7b", 4), ("chain", 1), ("s3b", 1), ("bn1", 0), ("aggr", 0), ("s4", 2), ("e2", 0), ("lateq", 0), ("tr", -3), ("ub", 3), ("wut", 0), ("q", -2), ("s5", 3), ("s9", 4), ("wur", 0),
 ]
 
 
@@ -120,15 +123,18 @@ def tile_graphmodel_pa_t_kernel(tc, x, edge, WA, WB, WE, WU, WV, out_0, out_1):
 
         ech = {}
 
+        def load_e1(jc, h):
+            t = stage.tile([P, 2, C], BF16, name="ech", tag="ech", bufs=6)
+            nc.sync.dma_start(out=t[:], in_=ev[h][:, 2 * jc : 2 * jc + 2, :])
+            ech[(h, jc)] = t
+
         def load_e(jc):
             for h in range(2):
-                t = stage.tile([P, 2, C], BF16, name="ech", tag="ech", bufs=6)
-                nc.sync.dma_start(out=t[:], in_=ev[h][:, 2 * jc : 2 * jc + 2, :])
-                ech[(h, jc)] = t
+                load_e1(jc, h)
 
         for h in range(2):
             nc.sync.dma_start(out=xn[:, h, :], in_=xv[h])
-        load_e(0)
+        load_e1(0, 0)
 
         gwt = {}
 
@@ -405,18 +411,17 @@ def tile_graphmodel_pa_t_kernel(tc, x, edge, WA, WB, WE, WU, WV, out_0, out_1):
                         scales=xs[:].rearrange("q h g r -> q (h g r)"),
                         in_=gx[:].rearrange("q h g w -> q (h g w)"),
                     )
-                    for t in range(2):
-                        st_tr(t, "acc", 4)
-                        st_evac(t)
+                    st_tr(0, "acc", 4)
+                    st_evac(0)
                     for jj in range(4):
                         xrep_copy(0, jj, False)
-                    for t in range(2):
-                        st_q(t)
+                    st_q(0)
                     xrep_quant(0)
                     st_tr(2)
                 prep_w(w, 2 * n2, start_tags)
                 prep_w(w, 2 * n2 + 1, start_tags)
                 quant_w(w, n2)
+        load_e1(0, 1)
         load_e(1)
         for a in range(4):
             load_w("WV", a)
@@ -433,8 +438,8 @@ def tile_graphmodel_pa_t_kernel(tc, x, edge, WA, WB, WE, WU, WV, out_0, out_1):
                         mx(u_[:], xc[:, h, g, :], xs[:, h, g, :], wc["WU"][:, g, cols], ws["WU"][:, g, cols], g == 0, g == 1)
                     uix[(h, n2)] = u_
 
-        late_p = {0: [("WV", 0), ("WV", 1)], 1: [("WV", 2), ("WV", 3)]}
-        late_q = {1: ("WV", 0), 2: ("WV", 1), WU_K0 + 8: ("WU", 0), WU_K0 + 16: ("WU", 1)}
+        late_u = WV_UNITS
+        late_q = {WV_Q[0]: ("WV", 0), WV_Q[1]: ("WV", 1), WU_K0 + 8: ("WU", 0), WU_K0 + 16: ("WU", 1)}
 
         def wu_unit(k):
             u = (k - WU_K0) // 2
@@ -492,9 +497,16 @@ def tile_graphmodel_pa_t_kernel(tc, x, edge, WA, WB, WE, WU, WV, out_0, out_1):
                     xrep_copy(a, k - (8 * a - 7), True)
                 if k == 8 * a - 3:
                     xrep_quant(a)
-            for w, a in late_p.get(k, []):
-                prep_w(w, a, [("ub", 2)] if k < 2 else [("acc", 4)])
-            if k == 1:
+            if k == 0:
+                st_tr(1, "ub", 2)
+                st_evac(1)
+                st_q(1)
+            for u in late_u.get(k, []):
+                if u % 4 == 0:
+                    new_gw("WV", u // 4)
+                unit_t("WV", u // 2, u % 2, "ub", 2)
+                unit_r("WV", u // 2, u % 2)
+            if k == 3:
                 for a in range(4):
                     load_w("WU", a)
             if k >= 3 and (k + 9 - s4lag) % 4 == 0 and 3 <= (k + 9 - s4lag) // 4 < 8:
@@ -510,32 +522,34 @@ def tile_graphmodel_pa_t_kernel(tc, x, edge, WA, WB, WE, WU, WV, out_0, out_1):
             st_s3(NT - 1, 0)
             st_s3(NT - 1, 1)
             st_chain(NT - 1)
-            for t in (NT - 4, NT - 3):
-                st_s8(t)
-                st_s7(t, 0)
-                st_s7(t, 1)
-                st_s6(t + 1)
-                st_s9(t)
-                st_s5(t + 2)
-                if t == NT - 4:
-                    st_s4(NT - 1)
+            st_s8(NT - 4)
+            st_s7(NT - 4, 0)
+            st_s7(NT - 4, 1)
+            st_s6(NT - 3)
+            st_s9(NT - 4)
+            st_s5(NT - 2)
+            st_s4(NT - 1)
+            st_s8(NT - 3)
+            st_s6(NT - 2)
+            st_s5(NT - 1)
+            st_s8(NT - 2)
+            st_s7(NT - 3, 0)
+            st_s7(NT - 3, 1)
             st_ub(NJ - 1)
             st_uix()
-            st_s8(NT - 2)
             st_s6(NT - 1)
-            st_s7(NT - 2, 0)
-            st_s7(NT - 2, 1)
             st_s8(NT - 1)
-            st_s9(NT - 2)
-            st_s7(NT - 1, 0)
-            st_s7(NT - 1, 1)
-            st_s9(NT - 1)
+            st_s9(NT - 3)
+            for t in (NT - 2, NT - 1):
+                st_s7(t, 0)
+                st_s7(t, 1)
+                st_s9(t)
 
         units = [(h, n2) for h in range(2) for n2 in range(2)]
         xnew = {}
         rdt = {}
         for h in range(2):
-            rdt[h] = work.tile([P, C], F32, name="rd", tag="te", bufs=TE_BUFS)
+            rdt[h] = den[h]
             xnew[h] = work.tile([P, C], F32, name="xnew", tag="rz", bufs=RZ_BUFS)
         for h, n2 in units:
             cols = slice(n2 * HALF, (n2 + 1) * HALF)
@@ -545,7 +559,8 @@ def tile_graphmodel_pa_t_kernel(tc, x, edge, WA, WB, WE, WU, WV, out_0, out_1):
             nc.scalar.activation(out=rdt[h][:, cols], in_=rdt[h][:, cols], func=ACTF.Exp, scale=-1.0)
         def tail_mul(h, n2):
             cols = slice(n2 * HALF, (n2 + 1) * HALF)
-            nc.vector.tensor_tensor(out=num[h][:, cols], in0=num[h][:, cols], in1=rdt[h][:, cols], op=ALU.mult)
+            eng = nc.gpsimd if (h == 1 and TAIL_POOL) else nc.vector
+            eng.tensor_tensor(out=num[h][:, cols], in0=num[h][:, cols], in1=rdt[h][:, cols], op=ALU.mult)
 
         def tail_add(h, n2):
             cols = slice(n2 * HALF, (n2 + 1) * HALF)

@@ -20,7 +20,7 @@ HALF = 512
 EPS = 1e-5
 FLOPS = 2 * 1024 * 1024 * (4096 + 4 * 256)
 
-PIN = True
+PIN = False
 S9_POOL_EVERY = 0
 S8_ON_DVE = False
 RZ_BUFS = 5

@@ -20,20 +20,7 @@ HALF = 512
 EPS = 1e-5
 FLOPS = 2 * 1024 * 1024 * (4096 + 4 * 256)
 
-PIN = False
-S9_POOL_EVERY = 0
-S8_ON_DVE = False
-RZ_BUFS = 5
-TE_BUFS = 3
-MT_BUFS = 2
-WU_K0 = 8
-WV_UNITS = {0: [0, 1, 2, 3], 1: [4, 5, 6, 7]}
-WV_Q = (1, 2)
-EPI = True
-TAIL_POOL = True
-SCHED = [
-    ("s6", 4), ("evac", -2), ("c0", 0), ("bn0", 0), ("stat", 1), ("s7a", 4), ("s8", 4), ("nm", 1), ("s3a", 1), ("c1", 0), ("s7b", 4), ("chain", 1), ("s3b", 1), ("bn1", 0), ("aggr", 0), ("s4", 2), ("e2", 0), ("lateq", 0), ("tr", -3), ("ub", 3), ("wut", 0), ("q", -2), ("s5", 3), ("s9", 4), ("wur", 0),
-]
+WU_FIRST_ROUND = 8
 
 
 def tile_graphmodel_pa_t_kernel(tc, x, edge, WA, WB, WE, WU, WV, out_0, out_1):
@@ -44,8 +31,7 @@ def tile_graphmodel_pa_t_kernel(tc, x, edge, WA, WB, WE, WU, WV, out_0, out_1):
         work = ctx.enter_context(tc.tile_pool(name="work", bufs=2))
         small = ctx.enter_context(tc.tile_pool(name="small", bufs=3))
         psum = ctx.enter_context(tc.psum_pool(name="psum", bufs=1))
-        if PIN:
-            ctx.enter_context(tc.manual_schedule())
+        ctx.enter_context(tc.manual_schedule())
 
         xv = x.flatten_outer_dims().rearrange("(p h) c -> h p c", h=2)
         o0 = out_0.flatten_outer_dims().rearrange("(p h) c -> h p c", h=2)
@@ -137,7 +123,6 @@ def tile_graphmodel_pa_t_kernel(tc, x, edge, WA, WB, WE, WU, WV, out_0, out_1):
         load_e1(0, 0)
 
         gwt = {}
-
         ubank = {}
 
         def unit_t(w, a, r2, tag, bufs):
@@ -170,7 +155,7 @@ def tile_graphmodel_pa_t_kernel(tc, x, edge, WA, WB, WE, WU, WV, out_0, out_1):
 
         grxt = {}
 
-        def xrep_copy(a, jj, on_act):
+        def xrep_copy(a, jj, on_scalar):
             if jj == 0:
                 grxt[a] = stage.tile([P, 4, 2, 512], BF16, name="grx", tag="gw", bufs=3, align_bytes=64)
             grf = grxt[a][:].bitcast(F32)
@@ -179,27 +164,66 @@ def tile_graphmodel_pa_t_kernel(tc, x, edge, WA, WB, WE, WU, WV, out_0, out_1):
             for g in range(2):
                 src = gxf[:, j % 2, g, :].rearrange("q (b l u) -> q b l u", b=16, l=8)[:, :, j // 2, :]
                 dst = grf[:, jj, g, :].rearrange("q (b i u) -> q b i u", b=16, i=8)
-                if on_act:
+                if on_scalar:
                     nc.scalar.copy(out=dst, in_=src.unsqueeze(2).to_broadcast([P, 16, 8, 2]))
                 else:
                     nc.vector.tensor_copy(out=dst, in_=src.unsqueeze(2).to_broadcast([P, 16, 8, 2]))
 
         def xrep_quant(a):
-            grx = grxt[a]
             nc.vector.quantize_mx(
                 out=xrc[:, 4 * a : 4 * a + 4, :, :].rearrange("q j g r -> q (j g r)").bitcast(FP8X4),
                 scales=xrs[:, 4 * a : 4 * a + 4, :, :].rearrange("q j g r -> q (j g r)"),
-                in_=grx[:].rearrange("q j g w -> q (j g w)"),
+                in_=grxt[a][:].rearrange("q j g w -> q (j g w)"),
             )
 
-        ge = {}
-        ecs = {}
-        trb = {}
-        acc = {}
-        stt_ = {}
+        bstt = {}
+        mvt = {}
+        pst = {}
         nmt = {}
         rstd = {}
+        nbt = {}
+
+        def stats_bn(key, n2, src):
+            if n2 == 0:
+                bstt[key] = small.tile([P, 12], F32, name="bst", tag="bst", bufs=3)
+            nc.vector.bn_stats(out=bstt[key][:, 6 * n2 : 6 * n2 + 6], in_=src)
+
+        def stats_aggr(key):
+            mvt[key] = small.tile([P, 3], F32, name="mv", tag="mv", bufs=3)
+            nc.vector.bn_aggr(out=mvt[key][:, 0:2], in_=bstt[key][:])
+
+        def stats_e2(key):
+            mv = mvt[key]
+            nc.vector.tensor_scalar(
+                out=mv[:, 2:3], in0=mv[:, 0:1], scalar1=mv[:, 0:1], scalar2=mv[:, 1:2], op0=ALU.mult, op1=ALU.add
+            )
+
+        def stats_sum(key):
+            pst[key] = psum.tile([P, HALF], F32, name="st", tag="st", bufs=1)
+            nc.tensor.matmul(out=pst[key][:, 0:3], lhsT=negg[:], rhs=mvt[key][:], start=True, stop=True)
+
+        def stats_out(key):
+            nmt[key] = small.tile([P, 3], F32, name="nm", tag="nm", bufs=4)
+            nc.scalar.copy(out=nmt[key][:], in_=pst[key][:, 0:3])
+
+        def stats_rstd(key, want_nb=False):
+            nm = nmt[key]
+            t1 = small.tile([P, 1], F32, name="t1", tag="t1", bufs=3)
+            nc.scalar.activation(out=t1[:], in_=nm[:, 0:1], func=ACTF.Identity, scale=nm[:, 0:1], bias=nm[:, 2:3])
+            u1 = small.tile([P, 1], F32, name="u1", tag="u1", bufs=3)
+            nc.scalar.activation(out=u1[:], in_=t1[:], func=ACTF.Identity, scale=-1.0, bias=epst[:, 0:1])
+            rstd[key] = small.tile([P, 1], F32, name="rstd", tag="rstd", bufs=4)
+            nc.gpsimd.tensor_tensor(out=rstd[key][:], in0=u1[:], in1=mhalf[:], op=ALU.pow)
+            if want_nb:
+                nbt[key] = small.tile([P, 1], F32, name="nb", tag="nb", bufs=2)
+                nc.gpsimd.tensor_tensor(out=nbt[key][:], in0=nm[:, 0:1], in1=rstd[key][:], op=ALU.mult)
+
+        trb = {}
+        ge = {}
+        ecs = {}
+        acc = {}
         rz = {}
+        tet = {}
         et = {}
         mt = {}
         ubt = {}
@@ -207,20 +231,20 @@ def tile_graphmodel_pa_t_kernel(tc, x, edge, WA, WB, WE, WU, WV, out_0, out_1):
         def ok(t):
             return 0 <= t < NT
 
-        def st_tr(t, tag="tr", bufs=1):
+        def t_transpose(t, tag="tr", bufs=1):
             if not ok(t):
                 return
             j, h = t // 2, t % 2
             ef = ech[(h, j // 2)][:].bitcast(F32)
             trb[t] = transposes(ef[:, j % 2, :], tag, bufs)
 
-        def st_evac(t):
+        def t_regroup(t):
             if not ok(t):
                 return
             ge[t] = stage.tile([P, 2, 512], BF16, name="ge", tag="ge", bufs=3, align_bytes=64)
             regroup(ge[t][:].bitcast(F32).rearrange("q g (r u) -> q g r u", u=2), trb[t])
 
-        def st_q(t):
+        def t_quantise(t):
             if not ok(t):
                 return
             c_ = stage.tile([P, 2, P], U32, name="ec", tag="ec", bufs=4, align_bytes=64)
@@ -232,7 +256,7 @@ def tile_graphmodel_pa_t_kernel(tc, x, edge, WA, WB, WE, WU, WV, out_0, out_1):
             )
             ecs[t] = (c_, s_)
 
-        def st_c(t, n2):
+        def t_agg(t, n2):
             if not ok(t):
                 return
             j, h = t // 2, t % 2
@@ -251,85 +275,41 @@ def tile_graphmodel_pa_t_kernel(tc, x, edge, WA, WB, WE, WU, WV, out_0, out_1):
                     mx(a_[:], lc[:, g, :], ls[:, g, :], wc[w][:, g, cols], ws[w][:, g, cols], i == 0, i == 5)
                     i += 1
 
-        bstt = {}
-
-        def stats_a1(key, n2, src):
-            if n2 == 0:
-                bstt[key] = small.tile([P, 12], F32, name="bst", tag="bst", bufs=3)
-            nc.vector.bn_stats(out=bstt[key][:, 6 * n2 : 6 * n2 + 6], in_=src)
-
-        def stats_a2(key):
-            mv = small.tile([P, 3], F32, name="mv", tag="mv", bufs=3)
-            nc.vector.bn_aggr(out=mv[:, 0:2], in_=bstt[key][:])
-            stt_[key] = mv
-
-        def stats_a3(key):
-            mv = stt_[key]
-            nc.vector.tensor_scalar(
-                out=mv[:, 2:3], in0=mv[:, 0:1], scalar1=mv[:, 0:1], scalar2=mv[:, 1:2], op0=ALU.mult, op1=ALU.add
-            )
-
-        def stats_b(key):
-            ps = psum.tile([P, HALF], F32, name="st", tag="st", bufs=1)
-            nc.tensor.matmul(out=ps[:, 0:3], lhsT=negg[:], rhs=stt_[key][:], start=True, stop=True)
-            stt_[key] = ps
-
-        def stats_c(key):
-            nm = small.tile([P, 3], F32, name="nm", tag="nm", bufs=4)
-            nc.scalar.copy(out=nm[:], in_=stt_[key][:, 0:3])
-            nmt[key] = nm
-
-        nbt = {}
-
-        def stats_d(key, want_nb=False):
-            nm = nmt[key]
-            t1 = small.tile([P, 1], F32, name="t1", tag="t1", bufs=3)
-            nc.scalar.activation(out=t1[:], in_=nm[:, 0:1], func=ACTF.Identity, scale=nm[:, 0:1], bias=nm[:, 2:3])
-            u1 = small.tile([P, 1], F32, name="u1", tag="u1", bufs=3)
-            nc.scalar.activation(out=u1[:], in_=t1[:], func=ACTF.Identity, scale=-1.0, bias=epst[:, 0:1])
-            rs = small.tile([P, 1], F32, name="rstd", tag="rstd", bufs=4)
-            nc.gpsimd.tensor_tensor(out=rs[:], in0=u1[:], in1=mhalf[:], op=ALU.pow)
-            rstd[key] = rs
-            if want_nb:
-                nb = small.tile([P, 1], F32, name="nb", tag="nb", bufs=2)
-                nc.gpsimd.tensor_tensor(out=nb[:], in0=nm[:, 0:1], in1=rs[:], op=ALU.mult)
-                nbt[key] = nb
-
-        def st_bn(t, n2):
+        def t_bn(t, n2):
             if ok(t):
-                stats_a1(t, n2, acc[(t, n2)][:])
+                stats_bn(t, n2, acc[(t, n2)][:])
 
-        def st_aggr(t):
+        def t_aggr(t):
             if ok(t):
-                stats_a2(t)
+                stats_aggr(t)
 
-        def st_e2(t):
+        def t_e2(t):
             if ok(t):
-                stats_a3(t)
+                stats_e2(t)
 
-        def st_stat(t):
+        def t_sum(t):
             if ok(t):
-                stats_b(t)
+                stats_sum(t)
 
-        def st_nm(t):
+        def t_out(t):
             if ok(t):
-                stats_c(t)
+                stats_out(t)
 
-        def st_chain(t):
+        def t_rstd(t):
             if ok(t):
-                stats_d(t)
+                stats_rstd(t)
 
-        def st_s3(t, n2):
+        def t_relu(t, n2):
             if not ok(t):
                 return
             if n2 == 0:
-                rz[t] = work.tile([P, C], F32, name="rz", tag="rz", bufs=RZ_BUFS)
+                rz[t] = work.tile([P, C], F32, name="rz", tag="rz", bufs=5)
             cols = slice(n2 * HALF, (n2 + 1) * HALF)
             nc.scalar.activation(
                 out=rz[t][:, cols], in_=acc[(t, n2)][:], func=ACTF.Relu, bias=nmt[t][:, 0:1], scale=1.0
             )
 
-        def st_s4(t):
+        def t_edge_out(t):
             if not ok(t):
                 return
             j, h = t // 2, t % 2
@@ -343,15 +323,13 @@ def tile_graphmodel_pa_t_kernel(tc, x, edge, WA, WB, WE, WU, WV, out_0, out_1):
             )
             nc.sync.dma_start(out=o1[h][:, j, :], in_=rz[t][:])
 
-        tet = {}
-
-        def st_s5(t):
+        def t_tanh(t):
             if not ok(t):
                 return
-            tet[t] = work.tile([P, C], F32, name="te", tag="te", bufs=TE_BUFS)
+            tet[t] = work.tile([P, C], F32, name="te", tag="te", bufs=3)
             nc.scalar.activation(out=tet[t][:], in_=rz[t][:], func=ACTF.Tanh, scale=0.5)
 
-        def st_s6(t):
+        def t_exp(t):
             if not ok(t):
                 return
             j, h = t // 2, t % 2
@@ -360,7 +338,7 @@ def tile_graphmodel_pa_t_kernel(tc, x, edge, WA, WB, WE, WU, WV, out_0, out_1):
             if t == NT - 1:
                 nc.scalar.activation(out=warm2[:], in_=epst[:], func=ACTF.Ln)
 
-        def st_ub(j):
+        def u_node(j):
             if not 0 <= j < NJ:
                 return
             for n2 in range(2):
@@ -370,30 +348,27 @@ def tile_graphmodel_pa_t_kernel(tc, x, edge, WA, WB, WE, WU, WV, out_0, out_1):
                     mx(u_[:], xrc[:, j, g, :], xrs[:, j, g, :], wc["WV"][:, g, cols], ws["WV"][:, g, cols], g == 0, g == 1)
                 ubt[(j, n2)] = u_
 
-        def st_s7(t, n2):
+        def t_prod(t, n2):
             if not ok(t):
                 return
             j, h = t // 2, t % 2
             if n2 == 0:
-                mt[t] = num[h] if j == 0 else work.tile([P, C], F32, name="mt", tag="mt", bufs=MT_BUFS)
+                mt[t] = num[h] if j == 0 else work.tile([P, C], F32, name="mt", tag="mt", bufs=2)
             cols = slice(n2 * HALF, (n2 + 1) * HALF)
             nc.vector.tensor_tensor(out=mt[t][:, cols], in0=et[t][:, cols], in1=ubt[(j, n2)][:], op=ALU.mult)
 
-        def st_s8(t):
+        def t_den(t):
             if not ok(t) or t < 2:
                 return
             h = t % 2
-            eng = nc.vector if (t >= NT - 4 or S8_ON_DVE) else nc.gpsimd
+            eng = nc.vector if t >= NT - 4 else nc.gpsimd
             eng.tensor_tensor(out=den[h][:], in0=den[h][:], in1=et[t][:], op=ALU.add)
 
-        def st_s9(t):
+        def t_num(t):
             if not ok(t) or t < 2:
                 return
             h = t % 2
-            eng = nc.vector
-            if S9_POOL_EVERY and t % S9_POOL_EVERY == 0:
-                eng = nc.gpsimd
-            eng.tensor_tensor(out=num[h][:], in0=num[h][:], in1=mt[t][:], op=ALU.add)
+            nc.vector.tensor_tensor(out=num[h][:], in0=num[h][:], in1=mt[t][:], op=ALU.add)
 
         start_tags = [("acc", 4), ("ub", 2)]
         for n2 in range(2):
@@ -411,13 +386,13 @@ def tile_graphmodel_pa_t_kernel(tc, x, edge, WA, WB, WE, WU, WV, out_0, out_1):
                         scales=xs[:].rearrange("q h g r -> q (h g r)"),
                         in_=gx[:].rearrange("q h g w -> q (h g w)"),
                     )
-                    st_tr(0, "acc", 4)
-                    st_evac(0)
+                    t_transpose(0, "acc", 4)
+                    t_regroup(0)
                     for jj in range(4):
                         xrep_copy(0, jj, False)
-                    st_q(0)
+                    t_quantise(0)
                     xrep_quant(0)
-                    st_tr(2)
+                    t_transpose(2)
                 prep_w(w, 2 * n2, start_tags)
                 prep_w(w, 2 * n2 + 1, start_tags)
                 quant_w(w, n2)
@@ -429,7 +404,7 @@ def tile_graphmodel_pa_t_kernel(tc, x, edge, WA, WB, WE, WU, WV, out_0, out_1):
 
         uix = {}
 
-        def st_uix():
+        def x_wu():
             for h in range(2):
                 for n2 in range(2):
                     u_ = psum.tile([P, HALF], F32, name="uix", tag="acc", bufs=4)
@@ -438,129 +413,114 @@ def tile_graphmodel_pa_t_kernel(tc, x, edge, WA, WB, WE, WU, WV, out_0, out_1):
                         mx(u_[:], xc[:, h, g, :], xs[:, h, g, :], wc["WU"][:, g, cols], ws["WU"][:, g, cols], g == 0, g == 1)
                     uix[(h, n2)] = u_
 
-        late_u = WV_UNITS
-        late_q = {WV_Q[0]: ("WV", 0), WV_Q[1]: ("WV", 1), WU_K0 + 8: ("WU", 0), WU_K0 + 16: ("WU", 1)}
-
         def wu_unit(k):
-            u = (k - WU_K0) // 2
-            if (k - WU_K0) % 2 != 0 or not 0 <= u < 8:
+            u = (k - WU_FIRST_ROUND) // 2
+            if (k - WU_FIRST_ROUND) % 2 != 0 or not 0 <= u < 8:
                 return None
-            return ("WU", u // 2, u % 2)
+            return (u // 2, u % 2)
 
-        stages = {
-            "c0": lambda t: st_c(t, 0),
-            "c1": lambda t: st_c(t, 1),
-            "bn0": lambda t: st_bn(t, 0),
-            "bn1": lambda t: st_bn(t, 1),
-            "aggr": st_aggr,
-            "e2": st_e2,
-            "stat": st_stat,
-            "nm": st_nm,
-            "chain": st_chain,
-            "s3a": lambda t: st_s3(t, 0),
-            "s3b": lambda t: st_s3(t, 1),
-            "s4": st_s4,
-            "s5": st_s5,
-            "s6": st_s6,
-            "s7a": lambda t: st_s7(t, 0),
-            "s7b": lambda t: st_s7(t, 1),
-            "s8": st_s8,
-            "s9": st_s9,
-            "q": st_q,
-            "evac": st_evac,
-            "tr": st_tr,
-        }
-        last = max(lag for name, lag in SCHED)
-        s4lag = dict(SCHED)["s4"]
-        for k in range(0, NT if EPI else NT + last + 1):
-            for name, lag in SCHED:
-                if name == "ub":
-                    if (k - lag) % 2 == 0:
-                        st_ub((k - lag) // 2)
-                elif name == "wut":
-                    un = wu_unit(k)
-                    if un is not None:
-                        if un[1] % 2 == 0 and un[2] == 0:
-                            new_gw("WU", un[1] // 2)
-                        unit_t(un[0], un[1], un[2], "st", 1)
-                elif name == "wur":
-                    un = wu_unit(k)
-                    if un is not None:
-                        unit_r(un[0], un[1], un[2])
-                elif name == "lateq":
-                    if k in late_q:
-                        quant_w(late_q[k][0], late_q[k][1])
-                else:
-                    stages[name](k - lag)
+        for k in range(NT):
+            t_exp(k - 4)
+            t_regroup(k + 2)
+            t_agg(k, 0)
+            t_bn(k, 0)
+            t_sum(k - 1)
+            t_prod(k - 4, 0)
+            t_den(k - 4)
+            t_out(k - 1)
+            t_relu(k - 1, 0)
+            t_agg(k, 1)
+            t_prod(k - 4, 1)
+            t_rstd(k - 1)
+            t_relu(k - 1, 1)
+            t_bn(k, 1)
+            t_aggr(k)
+            t_edge_out(k - 2)
+            t_e2(k)
+            if k in (1, 2):
+                quant_w("WV", k - 1)
+            if k in (WU_FIRST_ROUND + 8, WU_FIRST_ROUND + 16):
+                quant_w("WU", (k - WU_FIRST_ROUND) // 8 - 1)
+            t_transpose(k + 3)
+            if k % 2 == 1:
+                u_node((k - 3) // 2)
+            un = wu_unit(k)
+            if un is not None:
+                if un[0] % 2 == 0 and un[1] == 0:
+                    new_gw("WU", un[0] // 2)
+                unit_t("WU", un[0], un[1], "st", 1)
+            t_quantise(k + 2)
+            t_tanh(k - 3)
+            t_num(k - 4)
+            if un is not None:
+                unit_r("WU", un[0], un[1])
             for a in (1, 2, 3):
                 if 8 * a - 7 <= k <= 8 * a - 4:
                     xrep_copy(a, k - (8 * a - 7), True)
                 if k == 8 * a - 3:
                     xrep_quant(a)
             if k == 0:
-                st_tr(1, "ub", 2)
-                st_evac(1)
-                st_q(1)
-            for u in late_u.get(k, []):
-                if u % 4 == 0:
-                    new_gw("WV", u // 4)
-                unit_t("WV", u // 2, u % 2, "ub", 2)
-                unit_r("WV", u // 2, u % 2)
+                t_transpose(1, "ub", 2)
+                t_regroup(1)
+                t_quantise(1)
+            if k < 2:
+                for u in range(4 * k, 4 * k + 4):
+                    if u % 4 == 0:
+                        new_gw("WV", u // 4)
+                    unit_t("WV", u // 2, u % 2, "ub", 2)
+                    unit_r("WV", u // 2, u % 2)
             if k == 3:
                 for a in range(4):
                     load_w("WU", a)
-            if k >= 3 and (k + 9 - s4lag) % 4 == 0 and 3 <= (k + 9 - s4lag) // 4 < 8:
-                load_e((k + 9 - s4lag) // 4)
-            if k == NT + 2:
-                st_uix()
-        if EPI:
-            st_s6(NT - 4)
-            st_stat(NT - 1)
-            st_s4(NT - 2)
-            st_s5(NT - 3)
-            st_nm(NT - 1)
-            st_s3(NT - 1, 0)
-            st_s3(NT - 1, 1)
-            st_chain(NT - 1)
-            st_s8(NT - 4)
-            st_s7(NT - 4, 0)
-            st_s7(NT - 4, 1)
-            st_s6(NT - 3)
-            st_s9(NT - 4)
-            st_s5(NT - 2)
-            st_s4(NT - 1)
-            st_s8(NT - 3)
-            st_s6(NT - 2)
-            st_s5(NT - 1)
-            st_s8(NT - 2)
-            st_s7(NT - 3, 0)
-            st_s7(NT - 3, 1)
-            st_ub(NJ - 1)
-            st_uix()
-            st_s6(NT - 1)
-            st_s8(NT - 1)
-            st_s9(NT - 3)
-            for t in (NT - 2, NT - 1):
-                st_s7(t, 0)
-                st_s7(t, 1)
-                st_s9(t)
+            if k % 4 == 1 and 3 <= (k + 7) // 4 < NJ // 2:
+                load_e((k + 7) // 4)
+
+        t_exp(NT - 4)
+        t_sum(NT - 1)
+        t_edge_out(NT - 2)
+        t_tanh(NT - 3)
+        t_out(NT - 1)
+        t_relu(NT - 1, 0)
+        t_relu(NT - 1, 1)
+        t_rstd(NT - 1)
+        t_den(NT - 4)
+        t_prod(NT - 4, 0)
+        t_prod(NT - 4, 1)
+        t_exp(NT - 3)
+        t_num(NT - 4)
+        t_tanh(NT - 2)
+        t_edge_out(NT - 1)
+        t_den(NT - 3)
+        t_exp(NT - 2)
+        t_tanh(NT - 1)
+        t_den(NT - 2)
+        t_prod(NT - 3, 0)
+        t_prod(NT - 3, 1)
+        u_node(NJ - 1)
+        x_wu()
+        t_exp(NT - 1)
+        t_den(NT - 1)
+        t_num(NT - 3)
+        for t in (NT - 2, NT - 1):
+            t_prod(t, 0)
+            t_prod(t, 1)
+            t_num(t)
 
         units = [(h, n2) for h in range(2) for n2 in range(2)]
         xnew = {}
-        rdt = {}
         for h in range(2):
-            rdt[h] = den[h]
-            xnew[h] = work.tile([P, C], F32, name="xnew", tag="rz", bufs=RZ_BUFS)
+            xnew[h] = work.tile([P, C], F32, name="xnew", tag="rz", bufs=5)
         for h, n2 in units:
             cols = slice(n2 * HALF, (n2 + 1) * HALF)
-            nc.scalar.activation(out=rdt[h][:, cols], in_=den[h][:, cols], func=ACTF.Ln)
+            nc.scalar.activation(out=den[h][:, cols], in_=den[h][:, cols], func=ACTF.Ln)
         for h, n2 in units:
             cols = slice(n2 * HALF, (n2 + 1) * HALF)
-            nc.scalar.activation(out=rdt[h][:, cols], in_=rdt[h][:, cols], func=ACTF.Exp, scale=-1.0)
+            nc.scalar.activation(out=den[h][:, cols], in_=den[h][:, cols], func=ACTF.Exp, scale=-1.0)
+
         def tail_mul(h, n2):
             cols = slice(n2 * HALF, (n2 + 1) * HALF)
-            eng = nc.gpsimd if (h == 1 and TAIL_POOL) else nc.vector
-            eng.tensor_tensor(out=num[h][:, cols], in0=num[h][:, cols], in1=rdt[h][:, cols], op=ALU.mult)
+            eng = nc.gpsimd if h == 1 else nc.vector
+            eng.tensor_tensor(out=num[h][:, cols], in0=num[h][:, cols], in1=den[h][:, cols], op=ALU.mult)
 
         def tail_add(h, n2):
             cols = slice(n2 * HALF, (n2 + 1) * HALF)
@@ -575,29 +535,28 @@ def tile_graphmodel_pa_t_kernel(tc, x, edge, WA, WB, WE, WU, WV, out_0, out_1):
 
         def tail_bn(h, n2):
             cols = slice(n2 * HALF, (n2 + 1) * HALF)
-            stats_a1(("x", h), n2, xnew[h][:, cols])
+            stats_bn(("x", h), n2, xnew[h][:, cols])
 
         for f in (tail_mul, tail_add, tail_bn):
             f(0, 0)
             f(0, 1)
         tail_mul(1, 0)
-        stats_a2(("x", 0))
+        stats_aggr(("x", 0))
         tail_mul(1, 1)
-        stats_a3(("x", 0))
-        stats_b(("x", 0))
-        stats_c(("x", 0))
-        stats_d(("x", 0), True)
+        stats_e2(("x", 0))
+        stats_sum(("x", 0))
+        stats_out(("x", 0))
+        stats_rstd(("x", 0), True)
         for f in (tail_add, tail_bn):
             f(1, 0)
             f(1, 1)
-        stats_a2(("x", 1))
-        stats_a3(("x", 1))
-        stats_b(("x", 1))
-        stats_c(("x", 1))
-        stats_d(("x", 1), True)
+        stats_aggr(("x", 1))
+        stats_e2(("x", 1))
+        stats_sum(("x", 1))
+        stats_out(("x", 1))
+        stats_rstd(("x", 1), True)
         for h in range(2):
             key = ("x", h)
-            nb = nbt[key]
             for n2 in range(2):
                 cols = slice(n2 * HALF, (n2 + 1) * HALF)
                 nc.vector.scalar_tensor_tensor(
@@ -609,6 +568,6 @@ def tile_graphmodel_pa_t_kernel(tc, x, edge, WA, WB, WE, WU, WV, out_0, out_1):
                     op1=ALU.add,
                 )
                 nc.scalar.activation(
-                    out=xnew[h][:, cols], in_=xnew[h][:, cols], func=ACTF.Relu, bias=nb[:, 0:1], scale=1.0
+                    out=xnew[h][:, cols], in_=xnew[h][:, cols], func=ACTF.Relu, bias=nbt[key][:, 0:1], scale=1.0
                 )
                 nc.sync.dma_start(out=o0[h][:, cols], in_=xnew[h][:, cols])

from contextlib import ExitStack

import concourse.mybir as mybir
from concourse.masks import make_identity

F32 = mybir.dt.float32
BF16 = mybir.dt.bfloat16
U32 = mybir.dt.uint32
U8 = mybir.dt.uint8
FP8X4 = mybir.dt.float8_e4m3fn_x4
ALU = mybir.AluOpType
ACTF = mybir.ActivationFunctionType
AX = mybir.AxisListType

P = 128
C = 1024
NJ = 16
NT = 32
HALF = 512
EPS = 1e-5
FLOPS = 2 * 1024 * 1024 * (4096 + 4 * 256)

WU_FIRST_ROUND = 8


def tile_graphmodel_pa_t_kernel(tc, x, edge, WA, WB, WE, WU, WV, out_0, out_1):
    nc = tc.nc
    with ExitStack() as ctx:
        const = ctx.enter_context(tc.tile_pool(name="const", bufs=1))
        stage = ctx.enter_context(tc.tile_pool(name="stage", bufs=2))
        work = ctx.enter_context(tc.tile_pool(name="work", bufs=2))
        small = ctx.enter_context(tc.tile_pool(name="small", bufs=3))
        psum = ctx.enter_context(tc.psum_pool(name="psum", bufs=1))
        ctx.enter_context(tc.manual_schedule())

        xv = x.flatten_outer_dims().rearrange("(p h) c -> h p c", h=2)
        o0 = out_0.flatten_outer_dims().rearrange("(p h) c -> h p c", h=2)
        ev = edge.flatten_outer_dims().rearrange("(p h j) c -> h p j c", h=2, j=NJ)
        o1 = out_1.flatten_outer_dims().rearrange("(p h j) c -> h p j c", h=2, j=NJ)
        wdram = {"WA": WA, "WB": WB, "WE": WE, "WU": WU, "WV": WV}
        wview = {}
        for w in wdram:
            wview[w] = wdram[w].rearrange("(a r p) k -> a p r k", a=4, r=2)

        warm = const.tile([P, 1], F32, name="warm")
        nc.vector.memset(warm[:], 0.0)
        warm2 = const.tile([P, 1], F32, name="warm2")
        nc.scalar.activation(out=warm2[:], in_=warm[:], func=ACTF.Exp)
        mhalf = const.tile([P, 1], F32, name="mhalf")
        nc.vector.memset(mhalf[:], -0.5)
        epst = const.tile([P, 1], F32, name="epst")
        nc.vector.memset(epst[:], EPS)
        ident = const.tile([P, P], F32, name="ident")
        make_identity(nc, ident[:])
        rsel = const.tile([P, 8], F32, name="rsel")
        nc.vector.tensor_reduce(
            out=rsel[:], in_=ident[:].rearrange("p (a r) -> p r a", r=8), axis=AX.X, op=ALU.add
        )
        negg = const.tile([P, P], F32, name="negg")
        nc.vector.tensor_scalar(
            out=negg[:].rearrange("p (a r) -> p a r", r=8),
            in0=rsel[:].unsqueeze(1).to_broadcast([P, 16, 8]),
            scalar1=-1.0 / 16.0,
            scalar2=None,
            op0=ALU.mult,
        )

        wc = {}
        ws = {}
        for w in wdram:
            wc[w] = const.tile([P, 2, C], U32, name="wc" + w, align_bytes=64)
            ws[w] = const.tile([P, 2, C], U8, name="ws" + w, align_bytes=64)
        xn = const.tile([P, 2, C], BF16, name="xn")
        gx = const.tile([P, 2, 2, 512], BF16, name="gx", align_bytes=64)
        xc = const.tile([P, 2, 2, P], U32, name="xc", align_bytes=64)
        xs = const.tile([P, 2, 2, P], U8, name="xs", align_bytes=64)
        xrc = const.tile([P, NJ, 2, P], U32, name="xrc", align_bytes=64)
        xrs = const.tile([P, NJ, 2, P], U8, name="xrs", align_bytes=64)
        den = [const.tile([P, C], F32, name="den%d" % h) for h in range(2)]
        num = [const.tile([P, C], F32, name="num%d" % h) for h in range(2)]

        def transposes(src_f32, tag, bufs):
            bank = psum.tile([P, HALF], F32, name="bank_" + tag, tag=tag, bufs=bufs)
            for blk in range(4):
                cols = slice(blk * P, (blk + 1) * P)
                nc.tensor.transpose(bank[:, cols], src_f32[:, cols], ident[:])
            return bank

        def regroup(dst_f32, bank):
            nc.scalar.copy(out=dst_f32, in_=bank[:].rearrange("q (g u r) -> q g r u", g=2, u=2))

        def mx(out, lc, ls, rc, rs, start, stop):
            nc.tensor.matmul_mx(
                out=out,
                lhsT=lc.bitcast(FP8X4),
                lhsT_scale=ls,
                rhs=rc.bitcast(FP8X4),
                rhs_scale=rs,
                start=start,
                stop=stop,
            )

        wn = {}

        def load_w(w, a):
            t = stage.tile([P, 2, C], BF16, name="wn", tag="wn", bufs=4)
            nc.sync.dma_start(out=t[:], in_=wview[w][a])
            wn[(w, a)] = t

        ech = {}

        def load_e1(jc, h):
            t = stage.tile([P, 2, C], BF16, name="ech", tag="ech", bufs=6)
            nc.sync.dma_start(out=t[:], in_=ev[h][:, 2 * jc : 2 * jc + 2, :])
            ech[(h, jc)] = t

        def load_e(jc):
            for h in range(2):
                load_e1(jc, h)

        for h in range(2):
            nc.sync.dma_start(out=xn[:, h, :], in_=xv[h])
        load_e1(0, 0)

        gwt = {}
        ubank = {}

        def unit_t(w, a, r2, tag, bufs):
            ubank[(w, a, r2)] = transposes(wn[(w, a)][:].bitcast(F32)[:, r2, :], tag, bufs)

        def unit_r(w, a, r2):
            gwf = gwt[(w, a // 2)][:].bitcast(F32).rearrange("q g (r u) -> q g r u", u=2)
            r0 = ((a % 2) * 2 + r2) * P
            regroup(gwf[:, :, r0 : r0 + P, :], ubank[(w, a, r2)])

        def new_gw(w, n2):
            gwt[(w, n2)] = stage.tile([P, 2, 2048], BF16, name="gw", tag="gw", bufs=3, align_bytes=64)

        def prep_w(w, a, tags):
            if a % 2 == 0:
                new_gw(w, a // 2)
            for r2 in range(2):
                tag, bufs = tags[r2 % len(tags)]
                unit_t(w, a, r2, tag, bufs)
                unit_r(w, a, r2)

        def quant_w(w, n2):
            cols = slice(n2 * HALF, (n2 + 1) * HALF)
            for g in range(2):
                nc.vector.quantize_mx(
                    out=wc[w][:, g, cols].bitcast(FP8X4),
                    scales=ws[w][:, g, cols],
                    in_=gwt[(w, n2)][:, g, :],
                )

        grxt = {}

        def xrep_copy(a, jj, on_scalar):
            if jj == 0:
                grxt[a] = stage.tile([P, 4, 2, 512], BF16, name="grx", tag="gw", bufs=3, align_bytes=64)
            grf = grxt[a][:].bitcast(F32)
            gxf = gx[:].bitcast(F32)
            j = 4 * a + jj
            for g in range(2):
                src = gxf[:, j % 2, g, :].rearrange("q (b l u) -> q b l u", b=16, l=8)[:, :, j // 2, :]
                dst = grf[:, jj, g, :].rearrange("q (b i u) -> q b i u", b=16, i=8)
                if on_scalar:
                    nc.scalar.copy(out=dst, in_=src.unsqueeze(2).to_broadcast([P, 16, 8, 2]))
                else:
                    nc.vector.tensor_copy(out=dst, in_=src.unsqueeze(2).to_broadcast([P, 16, 8, 2]))

        def xrep_quant(a):
            nc.vector.quantize_mx(
                out=xrc[:, 4 * a : 4 * a + 4, :, :].rearrange("q j g r -> q (j g r)").bitcast(FP8X4),
                scales=xrs[:, 4 * a : 4 * a + 4, :, :].rearrange("q j g r -> q (j g r)"),
                in_=grxt[a][:].rearrange("q j g w -> q (j g w)"),
            )

        bstt = {}
        mvt = {}
        pst = {}
        nmt = {}
        rstd = {}
        nbt = {}

        def stats_bn(key, n2, src):
            if n2 == 0:
                bstt[key] = small.tile([P, 12], F32, name="bst", tag="bst", bufs=3)
            nc.vector.bn_stats(out=bstt[key][:, 6 * n2 : 6 * n2 + 6], in_=src)

        def stats_aggr(key):
            mvt[key] = small.tile([P, 3], F32, name="mv", tag="mv", bufs=3)
            nc.vector.bn_aggr(out=mvt[key][:, 0:2], in_=bstt[key][:])

        def stats_e2(key):
            mv = mvt[key]
            nc.vector.tensor_scalar(
                out=mv[:, 2:3], in0=mv[:, 0:1], scalar1=mv[:, 0:1], scalar2=mv[:, 1:2], op0=ALU.mult, op1=ALU.add
            )

        def stats_sum(key):
            pst[key] = psum.tile([P, HALF], F32, name="st", tag="st", bufs=1)
            nc.tensor.matmul(out=pst[key][:, 0:3], lhsT=negg[:], rhs=mvt[key][:], start=True, stop=True)

        def stats_out(key):
            nmt[key] = small.tile([P, 3], F32, name="nm", tag="nm", bufs=4)
            nc.scalar.copy(out=nmt[key][:], in_=pst[key][:, 0:3])

        def stats_rstd(key, want_nb=False):
            nm = nmt[key]
            t1 = small.tile([P, 1], F32, name="t1", tag="t1", bufs=3)
            nc.scalar.activation(out=t1[:], in_=nm[:, 0:1], func=ACTF.Identity, scale=nm[:, 0:1], bias=nm[:, 2:3])
            u1 = small.tile([P, 1], F32, name="u1", tag="u1", bufs=3)
            nc.scalar.activation(out=u1[:], in_=t1[:], func=ACTF.Identity, scale=-1.0, bias=epst[:, 0:1])
            rstd[key] = small.tile([P, 1], F32, name="rstd", tag="rstd", bufs=4)
            nc.gpsimd.tensor_tensor(out=rstd[key][:], in0=u1[:], in1=mhalf[:], op=ALU.pow)
            if want_nb:
                nbt[key] = small.tile([P, 1], F32, name="nb", tag="nb", bufs=2)
                nc.gpsimd.tensor_tensor(out=nbt[key][:], in0=nm[:, 0:1], in1=rstd[key][:], op=ALU.mult)

        trb = {}
        ge = {}
        ecs = {}
        acc = {}
        rz = {}
        tet = {}
        et = {}
        mt = {}
        ubt = {}

        def ok(t):
            return 0 <= t < NT

        def t_transpose(t, tag="tr", bufs=1):
            if not ok(t):
                return
            j, h = t // 2, t % 2
            ef = ech[(h, j // 2)][:].bitcast(F32)
            trb[t] = transposes(ef[:, j % 2, :], tag, bufs)

        def t_regroup(t):
            if not ok(t):
                return
            ge[t] = stage.tile([P, 2, 512], BF16, name="ge", tag="ge", bufs=3, align_bytes=64)
            regroup(ge[t][:].bitcast(F32).rearrange("q g (r u) -> q g r u", u=2), trb[t])

        def t_quantise(t):
            if not ok(t):
                return
            c_ = stage.tile([P, 2, P], U32, name="ec", tag="ec", bufs=4, align_bytes=64)
            s_ = stage.tile([P, 2, P], U8, name="es", tag="es", bufs=4, align_bytes=64)
            nc.vector.quantize_mx(
                out=c_[:].rearrange("q g r -> q (g r)").bitcast(FP8X4),
                scales=s_[:].rearrange("q g r -> q (g r)"),
                in_=ge[t][:].rearrange("q g w -> q (g w)"),
            )
            ecs[t] = (c_, s_)

        def t_agg(t, n2):
            if not ok(t):
                return
            j, h = t // 2, t % 2
            a_ = psum.tile([P, HALF], F32, name="acc", tag="acc", bufs=4)
            acc[(t, n2)] = a_
            cols = slice(n2 * HALF, (n2 + 1) * HALF)
            c_, s_ = ecs[t]
            ops = [
                (c_, s_, "WE"),
                (xc[:, h], xs[:, h], "WA"),
                (xrc[:, j], xrs[:, j], "WB"),
            ]
            i = 0
            for lc, ls, w in ops:
                for g in range(2):
                    mx(a_[:], lc[:, g, :], ls[:, g, :], wc[w][:, g, cols], ws[w][:, g, cols], i == 0, i == 5)
                    i += 1

        def t_bn(t, n2):
            if ok(t):
                stats_bn(t, n2, acc[(t, n2)][:])

        def t_aggr(t):
            if ok(t):
                stats_aggr(t)

        def t_e2(t):
            if ok(t):
                stats_e2(t)

        def t_sum(t):
            if ok(t):
                stats_sum(t)

        def t_out(t):
            if ok(t):
                stats_out(t)

        def t_rstd(t):
            if ok(t):
                stats_rstd(t)

        def t_relu(t, n2):
            if not ok(t):
                return
            if n2 == 0:
                rz[t] = work.tile([P, C], F32, name="rz", tag="rz", bufs=5)
            cols = slice(n2 * HALF, (n2 + 1) * HALF)
            nc.scalar.activation(
                out=rz[t][:, cols], in_=acc[(t, n2)][:], func=ACTF.Relu, bias=nmt[t][:, 0:1], scale=1.0
            )

        def t_edge_out(t):
            if not ok(t):
                return
            j, h = t // 2, t % 2
            nc.vector.scalar_tensor_tensor(
                out=rz[t][:],
                in0=rz[t][:],
                scalar=rstd[t][:, 0:1],
                in1=ech[(h, j // 2)][:, j % 2, :],
                op0=ALU.mult,
                op1=ALU.add,
            )
            nc.sync.dma_start(out=o1[h][:, j, :], in_=rz[t][:])

        def t_tanh(t):
            if not ok(t):
                return
            tet[t] = work.tile([P, C], F32, name="te", tag="te", bufs=3)
            nc.scalar.activation(out=tet[t][:], in_=rz[t][:], func=ACTF.Tanh, scale=0.5)

        def t_exp(t):
            if not ok(t):
                return
            j, h = t // 2, t % 2
            et[t] = den[h] if j == 0 else tet[t]
            nc.scalar.activation(out=et[t][:], in_=tet[t][:], func=ACTF.Exp, scale=0.5)
            if t == NT - 1:
                nc.scalar.activation(out=warm2[:], in_=epst[:], func=ACTF.Ln)

        def u_node(j):
            if not 0 <= j < NJ:
                return
            for n2 in range(2):
                u_ = psum.tile([P, HALF], F32, name="ub", tag="ub", bufs=2)
                cols = slice(n2 * HALF, (n2 + 1) * HALF)
                for g in range(2):
                    mx(u_[:], xrc[:, j, g, :], xrs[:, j, g, :], wc["WV"][:, g, cols], ws["WV"][:, g, cols], g == 0, g == 1)
                ubt[(j, n2)] = u_

        def t_prod(t, n2):
            if not ok(t):
                return
            j, h = t // 2, t % 2
            if n2 == 0:
                mt[t] = num[h] if j == 0 else work.tile([P, C], F32, name="mt", tag="mt", bufs=2)
            cols = slice(n2 * HALF, (n2 + 1) * HALF)
            nc.vector.tensor_tensor(out=mt[t][:, cols], in0=et[t][:, cols], in1=ubt[(j, n2)][:], op=ALU.mult)

        def t_den(t):
            if not ok(t) or t < 2:
                return
            h = t % 2
            eng = nc.vector if t >= NT - 4 else nc.gpsimd
            eng.tensor_tensor(out=den[h][:], in0=den[h][:], in1=et[t][:], op=ALU.add)

        def t_num(t):
            if not ok(t) or t < 2:
                return
            h = t % 2
            nc.vector.tensor_tensor(out=num[h][:], in0=num[h][:], in1=mt[t][:], op=ALU.add)

        start_tags = [("acc", 4), ("ub", 2)]
        for n2 in range(2):
            for w in ("WE", "WA", "WB"):
                load_w(w, 2 * n2)
                load_w(w, 2 * n2 + 1)
                if n2 == 0 and w == "WE":
                    gxf0 = gx[:].bitcast(F32)
                    xf = xn[:].bitcast(F32)
                    for h in range(2):
                        bank = transposes(xf[:, h, :], "acc", 4)
                        regroup(gxf0[:, h, :, :].rearrange("q g (r u) -> q g r u", u=2), bank)
                    nc.vector.quantize_mx(
                        out=xc[:].rearrange("q h g r -> q (h g r)").bitcast(FP8X4),
                        scales=xs[:].rearrange("q h g r -> q (h g r)"),
                        in_=gx[:].rearrange("q h g w -> q (h g w)"),
                    )
                    t_transpose(0, "acc", 4)
                    t_regroup(0)
                    for jj in range(4):
                        xrep_copy(0, jj, False)
                    t_quantise(0)
                    xrep_quant(0)
                    t_transpose(2)
                prep_w(w, 2 * n2, start_tags)
                prep_w(w, 2 * n2 + 1, start_tags)
                quant_w(w, n2)
        load_e1(0, 1)
        load_e(1)
        for a in range(4):
            load_w("WV", a)
        load_e(2)

        uix = {}

        def x_wu():
            for h in range(2):
                for n2 in range(2):
                    u_ = psum.tile([P, HALF], F32, name="uix", tag="acc", bufs=4)
                    cols = slice(n2 * HALF, (n2 + 1) * HALF)
                    for g in range(2):
                        mx(u_[:], xc[:, h, g, :], xs[:, h, g, :], wc["WU"][:, g, cols], ws["WU"][:, g, cols], g == 0, g == 1)
                    uix[(h, n2)] = u_

        def wu_unit(k):
            u = (k - WU_FIRST_ROUND) // 2
            if (k - WU_FIRST_ROUND) % 2 != 0 or not 0 <= u < 8:
                return None
            return (u // 2, u % 2)

        for k in range(NT):
            t_exp(k - 4)
            t_regroup(k + 2)
            t_agg(k, 0)
            t_bn(k, 0)
            t_sum(k - 1)
            t_prod(k - 4, 0)
            t_den(k - 4)
            t_out(k - 1)
            t_relu(k - 1, 0)
            t_agg(k, 1)
            t_prod(k - 4, 1)
            t_rstd(k - 1)
            t_relu(k - 1, 1)
            t_bn(k, 1)
            t_aggr(k)
            t_edge_out(k - 2)
            t_e2(k)
            if k in (1, 2):
                quant_w("WV", k - 1)
            if k in (WU_FIRST_ROUND + 8, WU_FIRST_ROUND + 16):
                quant_w("WU", (k - WU_FIRST_ROUND) // 8 - 1)
            t_transpose(k + 3)
            if k % 2 == 1:
                u_node((k - 3) // 2)
            un = wu_unit(k)
            if un is not None:
                if un[0] % 2 == 0 and un[1] == 0:
                    new_gw("WU", un[0] // 2)
                unit_t("WU", un[0], un[1], "st", 1)
            t_quantise(k + 2)
            t_tanh(k - 3)
            t_num(k - 4)
            if un is not None:
                unit_r("WU", un[0], un[1])
            for a in (1, 2, 3):
                if 8 * a - 7 <= k <= 8 * a - 4:
                    xrep_copy(a, k - (8 * a - 7), True)
                if k == 8 * a - 3:
                    xrep_quant(a)
            if k == 0:
                t_transpose(1, "ub", 2)
                t_regroup(1)
                t_quantise(1)
            if k < 2:
                for u in range(4 * k, 4 * k + 4):
                    if u % 4 == 0:
                        new_gw("WV", u // 4)
                    unit_t("WV", u // 2, u % 2, "ub", 2)
                    unit_r("WV", u // 2, u % 2)
            if k == 3:
                for a in range(4):
                    load_w("WU", a)
            if k % 4 == 1 and 3 <= (k + 7) // 4 < NJ // 2:
                load_e((k + 7) // 4)

        t_exp(NT - 4)
        t_sum(NT - 1)
        t_edge_out(NT - 2)
        t_tanh(NT - 3)
        t_out(NT - 1)
        t_relu(NT - 1, 0)
        t_relu(NT - 1, 1)
        t_rstd(NT - 1)
        t_den(NT - 4)
        t_prod(NT - 4, 0)
        t_prod(NT - 4, 1)
        t_exp(NT - 3)
        t_num(NT - 4)
        t_tanh(NT - 2)
        t_edge_out(NT - 1)
        t_den(NT - 3)
        t_exp(NT - 2)
        t_tanh(NT - 1)
        t_den(NT - 2)
        t_prod(NT - 3, 0)
        t_prod(NT - 3, 1)
        u_node(NJ - 1)
        x_wu()
        t_exp(NT - 1)
        t_den(NT - 1)
        t_num(NT - 3)
        for t in (NT - 2, NT - 1):
            t_prod(t, 0)
            t_prod(t, 1)
            t_num(t)

        units = [(h, n2) for h in range(2) for n2 in range(2)]
        xnew = {}
        for h in range(2):
            xnew[h] = work.tile([P, C], F32, name="xnew", tag="rz", bufs=5)
        for h, n2 in units:
            cols = slice(n2 * HALF, (n2 + 1) * HALF)
            nc.scalar.activation(out=den[h][:, cols], in_=den[h][:, cols], func=ACTF.Ln)
        for h, n2 in units:
            cols = slice(n2 * HALF, (n2 + 1) * HALF)
            nc.scalar.activation(out=den[h][:, cols], in_=den[h][:, cols], func=ACTF.Exp, scale=-1.0)

        def tail_mul(h, n2):
            cols = slice(n2 * HALF, (n2 + 1) * HALF)
            eng = nc.gpsimd if h == 1 else nc.vector
            eng.tensor_tensor(out=num[h][:, cols], in0=num[h][:, cols], in1=den[h][:, cols], op=ALU.mult)

        def tail_add(h, n2):
            cols = slice(n2 * HALF, (n2 + 1) * HALF)
            nc.vector.scalar_tensor_tensor(
                out=xnew[h][:, cols],
                in0=num[h][:, cols],
                scalar=1.0 / 16.0,
                in1=uix[(h, n2)][:],
                op0=ALU.mult,
                op1=ALU.add,
            )

        def tail_bn(h, n2):
            cols = slice(n2 * HALF, (n2 + 1) * HALF)
            stats_bn(("x", h), n2, xnew[h][:, cols])

        for f in (tail_mul, tail_add, tail_bn):
            f(0, 0)
            f(0, 1)
        tail_mul(1, 0)
        stats_aggr(("x", 0))
        tail_mul(1, 1)
        stats_e2(("x", 0))
        stats_sum(("x", 0))
        stats_out(("x", 0))
        stats_rstd(("x", 0), True)
        for f in (tail_add, tail_bn):
            f(1, 0)
            f(1, 1)
        stats_aggr(("x", 1))
        stats_e2(("x", 1))
        stats_sum(("x", 1))
        stats_out(("x", 1))
        stats_rstd(("x", 1), True)
        for h in range(2):
            key = ("x", h)
            for n2 in range(2):
                cols = slice(n2 * HALF, (n2 + 1) * HALF)
                nc.vector.scalar_tensor_tensor(
                    out=xnew[h][:, cols],
                    in0=xnew[h][:, cols],
                    scalar=rstd[key][:, 0:1],
                    in1=xn[:, h, cols],
                    op0=ALU.mult,
                    op1=ALU.add,
                )
                nc.scalar.activation(
                    out=xnew[h][:, cols], in_=xnew[h][:, cols], func=ACTF.Relu, bias=nbt[key][:, 0:1], scale=1.0
                )
                nc.sync.dma_start(out=o0[h][:, cols], in_=xnew[h][:, cols])
